import numpy as np
import ml_dtypes


def mxq(x, axis, fmt="e4m3"):
    dtype, down = {"e4m3": (ml_dtypes.float8_e4m3fn, 7), "e5m2": (ml_dtypes.float8_e5m2, 14)}[fmt]
    v = np.moveaxis(np.asarray(x, np.float32).astype(ml_dtypes.bfloat16).astype(np.float64), axis, -1)
    blocks = v.reshape(v.shape[:-1] + (-1, 32))
    amax = np.abs(blocks).max(-1, keepdims=True)
    byte = np.maximum(np.where(amax > 0, np.frexp(amax)[1] - 1 + 127, 0) - down, 1)
    scale = np.exp2(byte - 127.0)
    codes = (blocks / scale).astype(np.float32).astype(dtype).astype(np.float64)
    return np.moveaxis((codes * scale).reshape(v.shape), -1, axis)


WIDE = False


def mx_kscale(k):
    if not WIDE:
        return np.ones(k)
    levels = np.array([10, -10, 5, -5, 0])
    a = np.random.permutation(np.resize(levels, k // 512 * 4)).reshape(k // 512, 4)
    idx = np.arange(k)
    return np.exp2(a[idx // 512, idx % 128 // 32])


BF16 = ml_dtypes.bfloat16


def bf(x):
    return np.asarray(x, np.float32).astype(BF16)


def f64(x):
    return np.asarray(x).astype(np.float64)


E2M1 = np.array([0.0, 0.5, 1.0, 1.5, 2.0, 3.0, 4.0, 6.0, -0.0, -0.5, -1.0, -1.5, -2.0, -3.0, -4.0, -6.0])


def pack_weight(w, fmt):
    k, n = w.shape
    w = f64(bf(w)).reshape(k // 32, 32, n)
    amax = np.abs(w).max(1)
    if fmt == "e4m3":
        byte = np.frexp(amax)[1] - 1 + 127 - 7
    else:
        mant, ex = np.frexp(amax / 6.0)
        byte = np.where(mant > 0.5, ex, ex - 1) + 127
    byte = np.clip(np.where(amax > 0, byte, 1), 1, 254)
    scaled = (w * np.exp2(127.0 - byte)[:, None, :]).reshape(k, n).astype(np.float32)
    by_word = np.ascontiguousarray(scaled.reshape(k // 512, 128, 4, n).transpose(0, 1, 3, 2))
    if fmt == "e4m3":
        words = by_word.astype(ml_dtypes.float8_e4m3fn).view(np.uint8)
    else:
        c = by_word.astype(ml_dtypes.float4_e2m1fn).view(np.uint8) & 0xF
        words = c[..., 0::2] | (c[..., 1::2] << 4)
    return np.ascontiguousarray(words), np.ascontiguousarray(byte.astype(np.uint8).reshape(k // 512, 16, n))


def unpack_weight(words, scales, fmt):
    g, p, n, _ = words.shape
    if fmt == "e4m3":
        vals = np.ascontiguousarray(words).view(ml_dtypes.float8_e4m3fn).astype(np.float64)
    else:
        nib = np.empty((g, p, n, 4), np.uint8)
        nib[..., 0::2] = words & 0xF
        nib[..., 1::2] = words >> 4
        vals = E2M1[nib]
    vals = vals * np.repeat(np.exp2(scales.astype(np.float64) - 127.0), 8, axis=1)[..., None]
    return vals.transpose(0, 1, 3, 2).reshape(g * 512, n)

def pack4(w):
    words, scales = pack_weight(w, "e2m1")
    return words.reshape(words.shape[0], 128, -1), scales


def unpack4(words, scales):
    return unpack_weight(words.reshape(words.shape[0], 128, -1, 2), scales, "e2m1")


B, S, HID, NH, HD, RD, RATIO = 1, 2048, 1024, 8, 128, 64, 4
THETA = 10000.0
NW = S // RATIO
HALF = RD // 2


def rope_tables(positions):
    inv_freq = 1.0 / THETA ** (np.arange(HALF) / HALF)
    ang = positions[:, None] * inv_freq[None, :]
    return np.cos(ang), np.sin(ang)


def rope_interleaved(x, cos, sin):
    nope, rope = x[..., :-RD], x[..., -RD:]
    pr = rope.reshape(rope.shape[:-1] + (HALF, 2))
    a, b = pr[..., 0], pr[..., 1]
    new = np.stack([a * cos - b * sin, a * sin + b * cos], axis=-1).reshape(rope.shape)
    return np.concatenate([nope, new], axis=-1)


def remap(t, fill):
    cur = t[..., HD:]
    prev = np.concatenate([np.full((B, 1, RATIO, HD), fill), t[:, :-1, :, :HD]], axis=1)
    return np.concatenate([prev, cur], axis=2)


def pool_overlap(kv, gate, ape):
    kv_o = remap(kv.reshape(B, NW, RATIO, 2 * HD), 0.0)
    gate_o = remap(gate.reshape(B, NW, RATIO, 2 * HD) + ape, -np.inf)
    e = np.exp(gate_o - gate_o.max(axis=2, keepdims=True))
    w = e / e.sum(axis=2, keepdims=True)
    return (kv_o * w).sum(axis=2)


def setup_inputs():
    s = mx_kscale(HID)
    hidden = bf(np.random.standard_normal((B, S, HID)) * s)
    wkv_words, wkv_scales = pack4(np.random.standard_normal((HID, 2 * HD)) * 2.0 / np.sqrt(HID) / s[:, None])
    wgate_words, wgate_scales = pack4(np.random.standard_normal((HID, 2 * HD)) / np.sqrt(HID) / s[:, None])
    ape = bf(np.random.standard_normal((RATIO, 2 * HD)) * 0.5)
    return {"hidden": hidden,
            "wkv_words": wkv_words, "wkv_scales": wkv_scales,
            "wgate_words": wgate_words, "wgate_scales": wgate_scales,
            "ape": ape}


def reference(hidden, wkv_words, wkv_scales, wgate_words, wgate_scales, ape):
    hq = mxq(f64(hidden), 2, "e4m3")
    kv = hq @ unpack4(wkv_words, wkv_scales)
    gate = hq @ unpack4(wgate_words, wgate_scales)
    pooled = pool_overlap(kv, gate, f64(ape))
    ck, sk = rope_tables(np.arange(NW) * RATIO)
    k_rot = rope_interleaved(pooled, ck, sk)
    return k_rot, pooled

@@ -1,0 +1,330 @@
+import math
+from contextlib import ExitStack
+
+import concourse.mybir as mybir
+from concourse.masks import make_identity
+
+F32 = mybir.dt.float32
+BF16 = mybir.dt.bfloat16
+I32 = mybir.dt.int32
+U32 = mybir.dt.uint32
+U8 = mybir.dt.uint8
+FP8X4 = mybir.dt.float8_e4m3fn_x4
+FP4X4 = mybir.dt.float4_e2m1fn_x4
+ALU = mybir.AluOpType
+ACT = mybir.ActivationFunctionType
+
+P = 128
+TOKENS = 2048
+HIDDEN = 1024
+K_PASS = 512
+PASSES = HIDDEN // K_PASS
+SLOTS = 4
+SETS = 4
+ROPE = 64
+PAIRS = ROPE // 2
+THETA = 10000.0
+KV, GATE = 0, 1
+LO, HI = 0, 1
+MASKED = -1.0e30
+ROUND_TO_WHOLE = 1.5 * 2.0**23
+
+FLOPS = 2 * TOKENS * HIDDEN * 4 * P
+
+
+def tile_deepseekv4attention_pa_kernel(
+    tc, hidden, wkv_words, wkv_scales, wgate_words, wgate_scales, ape, out_0, out_1
+):
+    nc = tc.nc
+    with ExitStack() as stack:
+        keep = stack.enter_context(tc.tile_pool(name="keep", bufs=1))
+        stage = stack.enter_context(tc.tile_pool(name="stage", bufs=4))
+        work = stack.enter_context(tc.tile_pool(name="work", bufs=3))
+        psum_turn = stack.enter_context(tc.psum_pool(name="psum_turn", bufs=4))
+        psum_gate = stack.enter_context(tc.psum_pool(name="psum_gate", bufs=1))
+        psum_kv = stack.enter_context(tc.psum_pool(name="psum_kv", bufs=1))
+        stack.enter_context(tc.manual_schedule())
+
+        x = keep.tile([P, SETS * SLOTS, HIDDEN], BF16)
+        hidden_rows = hidden.rearrange("b (p i) k -> p (b i) k", i=SETS * SLOTS)
+
+        def load_tokens(first, count):
+            nc.sync.dma_start(out=x[:, first : first + count, :], in_=hidden_rows[:, first : first + count, :])
+
+        w_words = keep.tile([P, PASSES, 2, 4 * P], U8, align_bytes=64)
+        w_scales = keep.tile([P, PASSES, 2, 2 * P], U8, align_bytes=64)
+        nc.vector.memset(w_scales[:].bitcast(I32), 0)
+
+        def load_weight(which, words, scales):
+            nc.sync.dma_start(
+                out=w_words[:, :, which, :].bitcast(I32), in_=words.bitcast(I32).rearrange("g p b -> p g b")
+            )
+            rows = scales.bitcast(I32).rearrange("g q n -> q g n")
+            for quadrant in range(4):
+                nc.sync.dma_start(
+                    out=w_scales[32 * quadrant : 32 * quadrant + 4, :, which, :].bitcast(I32),
+                    in_=rows[4 * quadrant : 4 * quadrant + 4, :, :],
+                )
+
+        load_tokens(0, 2)
+        load_tokens(2, 2)
+        load_tokens(4, 4)
+        load_weight(GATE, wgate_words, wgate_scales)
+        load_tokens(8, 4)
+        load_tokens(12, 4)
+        load_weight(KV, wkv_words, wkv_scales)
+
+        window_int = keep.tile([P, SETS], I32)
+        nc.gpsimd.iota(window_int[:], pattern=[[1, SETS]], base=0, channel_multiplier=SETS)
+        ident = keep.tile([P, P], F32)
+        make_identity(nc, ident[:])
+        ape_rows = keep.tile([SLOTS, 2 * P], BF16)
+        nc.gpsimd.dma_start(out=ape_rows[:], in_=ape)
+
+        window = keep.tile([P, SETS], F32)
+        nc.vector.tensor_copy(out=window[:], in_=window_int[:])
+        freq = keep.tile([P, PAIRS], F32)
+        nc.vector.memset(freq[:, 0:1], 1.0)
+        have = 1
+        while have < PAIRS:
+            nc.vector.tensor_scalar_mul(
+                out=freq[:, have : 2 * have], in0=freq[:, 0:have], scalar1=THETA ** (-have / PAIRS)
+            )
+            have *= 2
+        table = [P, SETS, PAIRS]
+        turns = keep.tile(table, F32)
+        nc.vector.scalar_tensor_tensor(
+            out=turns[:],
+            in0=freq[:].unsqueeze(1).to_broadcast(table),
+            scalar=SLOTS / (2.0 * math.pi),
+            in1=window[:].unsqueeze(2).to_broadcast(table),
+            op0=ALU.mult,
+            op1=ALU.mult,
+        )
+        whole = keep.tile(table, F32)
+        nc.vector.tensor_scalar(
+            out=whole[:], in0=turns[:], scalar1=ROUND_TO_WHOLE, scalar2=ROUND_TO_WHOLE, op0=ALU.add, op1=ALU.subtract
+        )
+        part = keep.tile(table, F32)
+        nc.vector.tensor_tensor(out=part[:], in0=turns[:], in1=whole[:], op=ALU.subtract)
+        beyond = keep.tile(table, F32)
+        nc.vector.tensor_scalar(out=beyond[:], in0=part[:], scalar1=0.25, scalar2=None, op0=ALU.is_gt)
+        part_cos = keep.tile(table, F32)
+        nc.vector.scalar_tensor_tensor(
+            out=part_cos[:], in0=part[:], scalar=0.25, in1=beyond[:], op0=ALU.add, op1=ALU.subtract
+        )
+        cos_tab = keep.tile([P, SETS, PAIRS, 2], F32)
+        sin_tab = keep.tile([P, SETS, PAIRS, 2], F32)
+        full_turn = 2.0 * math.pi
+        nc.scalar.activation(out=sin_tab[:, :, :, 0], in_=part[:], func=ACT.Sin, scale=full_turn)
+        nc.scalar.activation(out=sin_tab[:, :, :, 1], in_=part[:], func=ACT.Sin, scale=-full_turn)
+        nc.scalar.activation(out=cos_tab[:, :, :, 0], in_=part_cos[:], func=ACT.Sin, scale=full_turn)
+        nc.scalar.activation(out=cos_tab[:, :, :, 1], in_=part_cos[:], func=ACT.Sin, scale=full_turn)
+
+        ape_wide = keep.tile([P, 2 * P], F32)
+        nc.vector.memset(ape_wide[:], 0.0)
+        ape_col = keep.tile([P, 2, SLOTS], F32)
+
+        def turn_ape():
+            nc.vector.tensor_copy(out=ape_wide[0:SLOTS, :], in_=ape_rows[:])
+            bank = psum_turn.tile([P, 2, 2, P], F32, tag="turn")
+            for half in (LO, HI):
+                nc.tensor.transpose(bank[:, 0, half, :], ape_wide[:, P * half : P * half + P], ident[:])
+            nc.vector.tensor_copy(out=ape_col[:], in_=bank[:, 0, :, 0:SLOTS])
+
+        codes = keep.tile([P, SETS, PASSES, SLOTS * P], U32, align_bytes=64)
+        planes = keep.tile([P, SETS, PASSES, SLOTS * P], U8, align_bytes=64)
+        x_words = x[:].bitcast(F32)
+        grouped = {}
+
+        def turn_set(a):
+            for g in range(PASSES):
+                grouped[a, g] = stage.tile([P, SLOTS * P, 4], BF16, align_bytes=64, name="grouped")
+                grouped_words = grouped[a, g][:].bitcast(F32)
+                for pair in range(2):
+                    bank = psum_turn.tile([P, 2, 2, P], F32, tag="turn")
+                    for u in range(2):
+                        for c in range(2):
+                            nc.tensor.transpose(
+                                bank[:, u, c, :],
+                                x_words[:, SLOTS * a + 2 * pair + c, 256 * g + u : 256 * (g + 1) : 2],
+                                ident[:],
+                            )
+                    target = grouped_words[:, 2 * P * pair : 2 * P * (pair + 1), :]
+                    source = bank[:].rearrange("q u c p -> q (c p) u")
+                    if a < 2 and pair == 1:
+                        nc.vector.tensor_copy(out=target, in_=source)
+                    else:
+                        nc.scalar.copy(out=target, in_=source)
+
+        def quantise_set(a):
+            for g in range(PASSES):
+                nc.vector.quantize_mx(
+                    out=codes[:, a, g, :].bitcast(FP8X4),
+                    scales=planes[:, a, g, :],
+                    in_=grouped[a, g][:].rearrange("q c t -> q (c t)"),
+                )
+
+        def project(pool, which, half, a, name):
+            bank = pool.tile([P, SLOTS, P], F32, name=name)
+            for g in range(PASSES):
+                nc.tensor.matmul_mx(
+                    out=bank[:].rearrange("f r p -> f (r p)"),
+                    lhsT=w_words[:, g, which, 2 * P * half : 2 * P * (half + 1)].bitcast(FP4X4),
+                    lhsT_scale=w_scales[:, g, which, P * half : P * (half + 1)],
+                    rhs=codes[:, a, g, :].bitcast(FP8X4),
+                    rhs_scale=planes[:, a, g, :],
+                    start=(g == 0),
+                    stop=(g == PASSES - 1),
+                )
+            return bank
+
+        gate, kv, top, below, both, one, pooled = {}, {}, {}, {}, {}, {}, {}
+        pooled_rows = keep.tile([P, SETS, P], F32)
+        rotated_rows = keep.tile([P, SETS, P], F32)
+        out_rotated = out_0.rearrange("b (p a) f -> p (b a) f", a=SETS)
+        out_pooled = out_1.rearrange("b (p a) f -> p (b a) f", a=SETS)
+
+        def skip(a):
+            return 1 if a == 0 else 0
+
+        def source(a, half):
+            return slice(0, P - skip(a)) if half == LO else slice(0, P)
+
+        def target(a, half):
+            return slice(skip(a), P) if half == LO else slice(0, P)
+
+        def project_gates(a):
+            gate[a] = {
+                LO: project(psum_gate, GATE, LO, (a - 1) % SETS, "gate_lo"),
+                HI: project(psum_gate, GATE, HI, a, "gate_hi"),
+            }
+
+        def project_kv(a):
+            kv[a] = {
+                LO: project(psum_kv, KV, LO, (a - 1) % SETS, "kv_lo"),
+                HI: project(psum_kv, KV, HI, a, "kv_hi"),
+            }
+
+        def find_top(a):
+            top[a] = work.tile([P, 2, P], F32, name="top")
+            for r in range(SLOTS):
+                for half in (LO, HI):
+                    best = top[a][:, half, target(a, half)]
+                    offset = ape_col[:, half, r : r + 1]
+                    if r == 0:
+                        nc.vector.tensor_scalar(
+                            out=best, in0=gate[a][half][:, r, source(a, half)], scalar1=offset, scalar2=None, op0=ALU.add
+                        )
+                    else:
+                        nc.vector.scalar_tensor_tensor(
+                            out=best,
+                            in0=gate[a][half][:, r, source(a, half)],
+                            scalar=offset,
+                            in1=best,
+                            op0=ALU.add,
+                            op1=ALU.max,
+                        )
+            shared = target(a, LO)
+            nc.vector.tensor_max(out=top[a][:, HI, shared], in0=top[a][:, HI, shared], in1=top[a][:, LO, shared])
+
+        def subtract_top(a):
+            below[a] = work.tile([P, 2 * SLOTS, P], F32, name="below")
+            if skip(a):
+                nc.vector.memset(below[a][:, 0:SLOTS, 0 : skip(a)], MASKED)
+            for half in (LO, HI):
+                nc.vector.tensor_tensor(
+                    out=below[a][:, SLOTS * half : SLOTS * (half + 1), target(a, half)],
+                    in0=gate[a][half][:, :, source(a, half)],
+                    in1=top[a][:, HI, target(a, half)]
+                    .unsqueeze(1)
+                    .to_broadcast([P, SLOTS, P - (skip(a) if half == LO else 0)]),
+                    op=ALU.subtract,
+                )
+
+        def weigh(a):
+            both[a] = work.tile([P, 2, 2 * SLOTS, P], F32, name="both")
+            for half in (LO, HI):
+                for r in range(SLOTS):
+                    nc.scalar.activation(
+                        out=both[a][:, 0, SLOTS * half + r, :],
+                        in_=below[a][:, SLOTS * half + r, :],
+                        func=ACT.Exp,
+                        bias=ape_col[:, half, r : r + 1],
+                        scale=1.0,
+                    )
+
+        def multiply(a):
+            if skip(a):
+                nc.vector.memset(both[a][:, 1, 0:SLOTS, 0 : skip(a)], 0.0)
+            for half in (LO, HI):
+                nc.vector.tensor_tensor(
+                    out=both[a][:, 1, SLOTS * half : SLOTS * (half + 1), target(a, half)],
+                    in0=kv[a][half][:, :, source(a, half)],
+                    in1=both[a][:, 0, SLOTS * half : SLOTS * (half + 1), target(a, half)],
+                    op=ALU.mult,
+                )
+
+        def add_slots(a, engine):
+            four = work.tile([P, 2, 4, P], F32, name="four")
+            engine.tensor_tensor(out=four[:], in0=both[a][:, :, 0:4, :], in1=both[a][:, :, 4:8, :], op=ALU.add)
+            two = work.tile([P, 2, 2, P], F32, name="two")
+            engine.tensor_tensor(out=two[:], in0=four[:, :, 0:2, :], in1=four[:, :, 2:4, :], op=ALU.add)
+            one[a] = work.tile([P, 2, P], F32, name="one")
+            engine.tensor_tensor(out=one[a][:], in0=two[:, :, 0, :], in1=two[:, :, 1, :], op=ALU.add)
+
+        def normalise(a):
+            inverse = work.tile([P, P], F32, name="inverse")
+            nc.vector.reciprocal(out=inverse[:], in_=one[a][:, 0, :])
+            pooled[a] = work.tile([P, P], F32, name="pooled")
+            nc.vector.tensor_tensor(out=pooled[a][:], in0=one[a][:, 1, :], in1=inverse[:], op=ALU.mult)
+
+        def finish(a):
+            bank = psum_turn.tile([P, 2, 2, P], F32, tag="turn")
+            nc.tensor.transpose(bank[:, 0, 0, :], pooled[a][:], ident[:])
+            nc.scalar.copy(out=pooled_rows[:, a, :], in_=bank[:, 0, 0, :])
+            nc.scalar.copy(out=rotated_rows[:, a, 0 : P - ROPE], in_=bank[:, 0, 0, 0 : P - ROPE])
+            nc.sync.dma_start(out=out_pooled[:, a, :], in_=pooled_rows[:, a, :])
+
+        def rotate(a, engine):
+            by_cos = work.tile([P, PAIRS, 2], F32, name="by_cos")
+            by_sin = work.tile([P, PAIRS, 2], F32, name="by_sin")
+            tail = pooled_rows[:, a, P - ROPE : P].rearrange("p (j e) -> p j e", e=2)
+            engine.tensor_tensor(out=by_cos[:], in0=tail, in1=cos_tab[:, a, :, :], op=ALU.mult)
+            engine.tensor_tensor(out=by_sin[:], in0=tail, in1=sin_tab[:, a, :, :], op=ALU.mult)
+            turned = rotated_rows[:, a, P - ROPE : P].rearrange("p (j e) -> p j e", e=2)
+            for e in range(2):
+                engine.tensor_tensor(out=turned[:, :, e], in0=by_cos[:, :, e], in1=by_sin[:, :, 1 - e], op=ALU.add)
+            nc.sync.dma_start(out=out_rotated[:, a, :], in_=rotated_rows[:, a, :])
+
+        units = [1, 2, 3, 0]
+        turn_set(0)
+        quantise_set(0)
+        turn_set(1)
+        turn_ape()
+        quantise_set(1)
+        warm = keep.tile([P, 1], F32)
+        nc.scalar.activation(out=warm[:], in_=freq[:, 0:1], func=ACT.Exp)
+        project_gates(units[0])
+        for s in range(SETS + 2):
+            if s + 2 < SETS:
+                turn_set(s + 2)
+            if s < SETS:
+                find_top(units[s])
+                subtract_top(units[s])
+            if s + 2 < SETS:
+                quantise_set(s + 2)
+            if s + 1 < SETS:
+                project_gates(units[s + 1])
+            if s < SETS:
+                weigh(units[s])
+            if 0 <= s - 1 < SETS:
+                multiply(units[s - 1])
+            if s < SETS:
+                project_kv(units[s])
+            if 0 <= s - 1 < SETS:
+                add_slots(units[s - 1], nc.gpsimd if s < SETS else nc.vector)
+            if 0 <= s - 2:
+                normalise(units[s - 2])
+                finish(units[s - 2])
+                rotate(units[s - 2], nc.gpsimd if s - 2 < SETS - 1 else nc.vector)

@@ -48,8 +48,10 @@ def tile_deepseekv4attention_pa_kernel(
         x = keep.tile([P, SETS * SLOTS, HIDDEN], BF16)
         hidden_rows = hidden.rearrange("b (p i) k -> p (b i) k", i=SETS * SLOTS)
 
-        def load_tokens(first, count):
-            nc.sync.dma_start(out=x[:, first : first + count, :], in_=hidden_rows[:, first : first + count, :])
+        def load_set(a):
+            nc.gpsimd.dma_start(
+                out=x[:, SLOTS * a : SLOTS * (a + 1), :], in_=hidden_rows[:, SLOTS * a : SLOTS * (a + 1), :]
+            )
 
         w_words = keep.tile([P, PASSES, 2, 4 * P], U8, align_bytes=64)
         w_scales = keep.tile([P, PASSES, 2, 2 * P], U8, align_bytes=64)
@@ -66,20 +68,19 @@ def tile_deepseekv4attention_pa_kernel(
                     in_=rows[4 * quadrant : 4 * quadrant + 4, :, :],
                 )
 
-        load_tokens(0, 2)
-        load_tokens(2, 2)
-        load_tokens(4, 4)
         load_weight(GATE, wgate_words, wgate_scales)
-        load_tokens(8, 4)
-        load_tokens(12, 4)
         load_weight(KV, wkv_words, wkv_scales)
+        ape_rows = keep.tile([SLOTS, 2 * P], BF16)
+        nc.sync.dma_start(out=ape_rows[:], in_=ape)
+        load_set(0)
+        load_set(1)
 
-        window_int = keep.tile([P, SETS], I32)
-        nc.gpsimd.iota(window_int[:], pattern=[[1, SETS]], base=0, channel_multiplier=SETS)
         ident = keep.tile([P, P], F32)
         make_identity(nc, ident[:])
-        ape_rows = keep.tile([SLOTS, 2 * P], BF16)
-        nc.gpsimd.dma_start(out=ape_rows[:], in_=ape)
+        load_set(2)
+        load_set(3)
+        window_int = keep.tile([P, SETS], I32)
+        nc.gpsimd.iota(window_int[:], pattern=[[1, SETS]], base=0, channel_multiplier=SETS)
 
         window = keep.tile([P, SETS], F32)
         nc.vector.tensor_copy(out=window[:], in_=window_int[:])

@@ -26,8 +26,10 @@ PAIRS = ROPE // 2
 THETA = 10000.0
 KV, GATE = 0, 1
 LO, HI = 0, 1
+WEIGHTS, PRODUCTS = 0, 1
 MASKED = -1.0e30
 ROUND_TO_WHOLE = 1.5 * 2.0**23
+BLOCK = 8
 
 FLOPS = 2 * TOKENS * HIDDEN * 4 * P
 
@@ -38,7 +40,6 @@ def tile_deepseekv4attention_pa_kernel(
     nc = tc.nc
     with ExitStack() as stack:
         keep = stack.enter_context(tc.tile_pool(name="keep", bufs=1))
-        stage = stack.enter_context(tc.tile_pool(name="stage", bufs=4))
         work = stack.enter_context(tc.tile_pool(name="work", bufs=3))
         psum_turn = stack.enter_context(tc.psum_pool(name="psum_turn", bufs=4))
         psum_gate = stack.enter_context(tc.psum_pool(name="psum_gate", bufs=1))
@@ -48,10 +49,9 @@ def tile_deepseekv4attention_pa_kernel(
         x = keep.tile([P, SETS * SLOTS, HIDDEN], BF16)
         hidden_rows = hidden.rearrange("b (p i) k -> p (b i) k", i=SETS * SLOTS)
 
-        def load_set(a):
-            nc.gpsimd.dma_start(
-                out=x[:, SLOTS * a : SLOTS * (a + 1), :], in_=hidden_rows[:, SLOTS * a : SLOTS * (a + 1), :]
-            )
+        def load_half_set(a, half):
+            first = SLOTS * a + 2 * half
+            nc.sync.dma_start(out=x[:, first : first + 2, :], in_=hidden_rows[:, first : first + 2, :])
 
         w_words = keep.tile([P, PASSES, 2, 4 * P], U8, align_bytes=64)
         w_scales = keep.tile([P, PASSES, 2, 2 * P], U8, align_bytes=64)
@@ -68,19 +68,22 @@ def tile_deepseekv4attention_pa_kernel(
                     in_=rows[4 * quadrant : 4 * quadrant + 4, :, :],
                 )
 
+        for a in (0, 1):
+            for half in range(2):
+                load_half_set(a, half)
         load_weight(GATE, wgate_words, wgate_scales)
+        for half in range(2):
+            load_half_set(2, half)
         load_weight(KV, wkv_words, wkv_scales)
-        ape_rows = keep.tile([SLOTS, 2 * P], BF16)
-        nc.sync.dma_start(out=ape_rows[:], in_=ape)
-        load_set(0)
-        load_set(1)
+        for half in range(2):
+            load_half_set(3, half)
 
-        ident = keep.tile([P, P], F32)
-        make_identity(nc, ident[:])
-        load_set(2)
-        load_set(3)
         window_int = keep.tile([P, SETS], I32)
         nc.gpsimd.iota(window_int[:], pattern=[[1, SETS]], base=0, channel_multiplier=SETS)
+        ident = keep.tile([P, P], F32)
+        make_identity(nc, ident[:])
+        ape_rows = keep.tile([SLOTS, 2 * P], BF16)
+        nc.gpsimd.dma_start(out=ape_rows[:], in_=ape)
 
         window = keep.tile([P, SETS], F32)
         nc.vector.tensor_copy(out=window[:], in_=window_int[:])
@@ -128,42 +131,39 @@ def tile_deepseekv4attention_pa_kernel(
 
         def turn_ape():
             nc.vector.tensor_copy(out=ape_wide[0:SLOTS, :], in_=ape_rows[:])
-            bank = psum_turn.tile([P, 2, 2, P], F32, tag="turn")
+            bank = psum_turn.tile([P, PASSES, 2, P], F32, tag="turn")
             for half in (LO, HI):
                 nc.tensor.transpose(bank[:, 0, half, :], ape_wide[:, P * half : P * half + P], ident[:])
             nc.vector.tensor_copy(out=ape_col[:], in_=bank[:, 0, :, 0:SLOTS])
 
+        x_words = x[:].bitcast(F32)
+        grouped = keep.tile([P, SETS, PASSES, SLOTS * P, 4], BF16, align_bytes=64)
+        grouped_words = grouped[:].bitcast(F32)
         codes = keep.tile([P, SETS, PASSES, SLOTS * P], U32, align_bytes=64)
         planes = keep.tile([P, SETS, PASSES, SLOTS * P], U8, align_bytes=64)
-        x_words = x[:].bitcast(F32)
-        grouped = {}
+
+        def turn_half_set(a, half):
+            for r in (2 * half, 2 * half + 1):
+                bank = psum_turn.tile([P, PASSES, 2, P], F32, tag="turn")
+                for g in range(PASSES):
+                    for u in range(2):
+                        nc.tensor.transpose(
+                            bank[:, g, u, :], x_words[:, SLOTS * a + r, 2 * P * g + u : 2 * P * (g + 1) : 2], ident[:]
+                        )
+                nc.scalar.copy(
+                    out=grouped_words[:, a, :, P * r : P * (r + 1), :], in_=bank[:].rearrange("q g u p -> q g p u")
+                )
 
         def turn_set(a):
-            for g in range(PASSES):
-                grouped[a, g] = stage.tile([P, SLOTS * P, 4], BF16, align_bytes=64, name="grouped")
-                grouped_words = grouped[a, g][:].bitcast(F32)
-                for pair in range(2):
-                    bank = psum_turn.tile([P, 2, 2, P], F32, tag="turn")
-                    for u in range(2):
-                        for c in range(2):
-                            nc.tensor.transpose(
-                                bank[:, u, c, :],
-                                x_words[:, SLOTS * a + 2 * pair + c, 256 * g + u : 256 * (g + 1) : 2],
-                                ident[:],
-                            )
-                    target = grouped_words[:, 2 * P * pair : 2 * P * (pair + 1), :]
-                    source = bank[:].rearrange("q u c p -> q (c p) u")
-                    if a < 2 and pair == 1:
-                        nc.vector.tensor_copy(out=target, in_=source)
-                    else:
-                        nc.scalar.copy(out=target, in_=source)
+            for half in range(2):
+                turn_half_set(a, half)
 
         def quantise_set(a):
             for g in range(PASSES):
                 nc.vector.quantize_mx(
                     out=codes[:, a, g, :].bitcast(FP8X4),
                     scales=planes[:, a, g, :],
-                    in_=grouped[a, g][:].rearrange("q c t -> q (c t)"),
+                    in_=grouped[:, a, g].rearrange("q c t -> q (c t)"),
                 )
 
         def project(pool, which, half, a, name):
@@ -180,7 +180,7 @@ def tile_deepseekv4attention_pa_kernel(
                 )
             return bank
 
-        gate, kv, top, below, both, one, pooled = {}, {}, {}, {}, {}, {}, {}
+        gate, kv, logit, both, halved, sums, inverse = {}, {}, {}, {}, {}, {}, {}
         pooled_rows = keep.tile([P, SETS, P], F32)
         rotated_rows = keep.tile([P, SETS, P], F32)
         out_rotated = out_0.rearrange("b (p a) f -> p (b a) f", a=SETS)
@@ -195,6 +195,9 @@ def tile_deepseekv4attention_pa_kernel(
         def target(a, half):
             return slice(skip(a), P) if half == LO else slice(0, P)
 
+        def slots(half):
+            return slice(SLOTS * half, SLOTS * (half + 1))
+
         def project_gates(a):
             gate[a] = {
                 LO: project(psum_gate, GATE, LO, (a - 1) % SETS, "gate_lo"),
@@ -207,87 +210,73 @@ def tile_deepseekv4attention_pa_kernel(
                 HI: project(psum_kv, KV, HI, a, "kv_hi"),
             }
 
-        def find_top(a):
-            top[a] = work.tile([P, 2, P], F32, name="top")
-            for r in range(SLOTS):
-                for half in (LO, HI):
-                    best = top[a][:, half, target(a, half)]
-                    offset = ape_col[:, half, r : r + 1]
-                    if r == 0:
-                        nc.vector.tensor_scalar(
-                            out=best, in0=gate[a][half][:, r, source(a, half)], scalar1=offset, scalar2=None, op0=ALU.add
-                        )
-                    else:
-                        nc.vector.scalar_tensor_tensor(
-                            out=best,
-                            in0=gate[a][half][:, r, source(a, half)],
-                            scalar=offset,
-                            in1=best,
-                            op0=ALU.add,
-                            op1=ALU.max,
-                        )
-            shared = target(a, LO)
-            nc.vector.tensor_max(out=top[a][:, HI, shared], in0=top[a][:, HI, shared], in1=top[a][:, LO, shared])
-
-        def subtract_top(a):
-            below[a] = work.tile([P, 2 * SLOTS, P], F32, name="below")
+        def add_offsets(a):
+            logit[a] = work.tile([P, 2 * SLOTS, P], F32, name="logit")
             if skip(a):
-                nc.vector.memset(below[a][:, 0:SLOTS, 0 : skip(a)], MASKED)
-            for half in (LO, HI):
-                nc.vector.tensor_tensor(
-                    out=below[a][:, SLOTS * half : SLOTS * (half + 1), target(a, half)],
-                    in0=gate[a][half][:, :, source(a, half)],
-                    in1=top[a][:, HI, target(a, half)]
-                    .unsqueeze(1)
-                    .to_broadcast([P, SLOTS, P - (skip(a) if half == LO else 0)]),
-                    op=ALU.subtract,
-                )
-
-        def weigh(a):
-            both[a] = work.tile([P, 2, 2 * SLOTS, P], F32, name="both")
+                nc.gpsimd.memset(logit[a][:, slots(LO), 0:BLOCK], MASKED)
             for half in (LO, HI):
                 for r in range(SLOTS):
                     nc.scalar.activation(
-                        out=both[a][:, 0, SLOTS * half + r, :],
-                        in_=below[a][:, SLOTS * half + r, :],
-                        func=ACT.Exp,
+                        out=logit[a][:, SLOTS * half + r, target(a, half)],
+                        in_=gate[a][half][:, r, source(a, half)],
+                        func=ACT.Identity,
                         bias=ape_col[:, half, r : r + 1],
                         scale=1.0,
                     )
 
+        def subtract_top(a):
+            four = work.tile([P, 4, P], F32, name="top_four")
+            nc.vector.tensor_max(out=four[:], in0=logit[a][:, 0:4, :], in1=logit[a][:, 4:8, :])
+            two = work.tile([P, 2, P], F32, name="top_two")
+            nc.vector.tensor_max(out=two[:], in0=four[:, 0:2, :], in1=four[:, 2:4, :])
+            top = work.tile([P, P], F32, name="top")
+            nc.vector.tensor_max(out=top[:], in0=two[:, 0, :], in1=two[:, 1, :])
+            nc.vector.tensor_tensor(
+                out=logit[a][:],
+                in0=logit[a][:],
+                in1=top[:].unsqueeze(1).to_broadcast([P, 2 * SLOTS, P]),
+                op=ALU.subtract,
+            )
+
+        def weigh(a):
+            both[a] = work.tile([P, 2, 2 * SLOTS, P], F32, name="both")
+            halved[a] = work.tile([P, 2, SLOTS, P], F32, name="halved")
+            nc.scalar.activation(out=both[a][:, WEIGHTS], in_=logit[a][:], func=ACT.Exp)
+
         def multiply(a):
             if skip(a):
-                nc.vector.memset(both[a][:, 1, 0:SLOTS, 0 : skip(a)], 0.0)
+                nc.vector.memset(both[a][:, PRODUCTS, slots(LO), 0 : skip(a)], 0.0)
             for half in (LO, HI):
                 nc.vector.tensor_tensor(
-                    out=both[a][:, 1, SLOTS * half : SLOTS * (half + 1), target(a, half)],
+                    out=both[a][:, PRODUCTS, slots(half), target(a, half)],
                     in0=kv[a][half][:, :, source(a, half)],
-                    in1=both[a][:, 0, SLOTS * half : SLOTS * (half + 1), target(a, half)],
+                    in1=both[a][:, WEIGHTS, slots(half), target(a, half)],
                     op=ALU.mult,
                 )
 
-        def add_slots(a, engine):
-            four = work.tile([P, 2, 4, P], F32, name="four")
-            engine.tensor_tensor(out=four[:], in0=both[a][:, :, 0:4, :], in1=both[a][:, :, 4:8, :], op=ALU.add)
-            two = work.tile([P, 2, 2, P], F32, name="two")
-            engine.tensor_tensor(out=two[:], in0=four[:, :, 0:2, :], in1=four[:, :, 2:4, :], op=ALU.add)
-            one[a] = work.tile([P, 2, P], F32, name="one")
-            engine.tensor_tensor(out=one[a][:], in0=two[:, :, 0, :], in1=two[:, :, 1, :], op=ALU.add)
+        def halve_slots(a, which, engine):
+            engine.tensor_tensor(
+                out=halved[a][:, which], in0=both[a][:, which, slots(LO), :], in1=both[a][:, which, slots(HI), :], op=ALU.add
+            )
 
-        def normalise(a):
-            inverse = work.tile([P, P], F32, name="inverse")
-            nc.vector.reciprocal(out=inverse[:], in_=one[a][:, 0, :])
-            pooled[a] = work.tile([P, P], F32, name="pooled")
-            nc.vector.tensor_tensor(out=pooled[a][:], in0=one[a][:, 1, :], in1=inverse[:], op=ALU.mult)
+        def add_and_turn(a, which):
+            bank = psum_turn.tile([P, PASSES, 2, P], F32, tag="turn", name="sums")
+            sums[a, which] = bank[:, 0, 0, :]
+            for s in range(SLOTS):
+                nc.tensor.matmul(
+                    out=sums[a, which], lhsT=halved[a][:, which, s, :], rhs=ident[:], start=(s == 0), stop=(s == SLOTS - 1)
+                )
 
-        def finish(a):
-            bank = psum_turn.tile([P, 2, 2, P], F32, tag="turn")
-            nc.tensor.transpose(bank[:, 0, 0, :], pooled[a][:], ident[:])
-            nc.scalar.copy(out=pooled_rows[:, a, :], in_=bank[:, 0, 0, :])
-            nc.scalar.copy(out=rotated_rows[:, a, 0 : P - ROPE], in_=bank[:, 0, 0, 0 : P - ROPE])
+        def invert(a):
+            inverse[a] = work.tile([P, P], F32, name="inverse")
+            nc.vector.reciprocal(out=inverse[a][:], in_=sums[a, WEIGHTS])
+
+        def divide(a):
+            nc.vector.tensor_tensor(out=pooled_rows[:, a, :], in0=sums[a, PRODUCTS], in1=inverse[a][:], op=ALU.mult)
             nc.sync.dma_start(out=out_pooled[:, a, :], in_=pooled_rows[:, a, :])
 
         def rotate(a, engine):
+            nc.scalar.copy(out=rotated_rows[:, a, 0 : P - ROPE], in_=pooled_rows[:, a, 0 : P - ROPE])
             by_cos = work.tile([P, PAIRS, 2], F32, name="by_cos")
             by_sin = work.tile([P, PAIRS, 2], F32, name="by_sin")
             tail = pooled_rows[:, a, P - ROPE : P].rearrange("p (j e) -> p j e", e=2)
@@ -300,32 +289,40 @@ def tile_deepseekv4attention_pa_kernel(
 
         units = [1, 2, 3, 0]
         turn_set(0)
-        quantise_set(0)
         turn_set(1)
+        quantise_set(0)
         turn_ape()
         quantise_set(1)
         warm = keep.tile([P, 1], F32)
         nc.scalar.activation(out=warm[:], in_=freq[:, 0:1], func=ACT.Exp)
         project_gates(units[0])
-        for s in range(SETS + 2):
-            if s + 2 < SETS:
-                turn_set(s + 2)
+        add_offsets(units[0])
+        turn_set(2)
+        project_kv(units[0])
+        for s in range(SETS + 1):
+            last = s == SETS - 1
+            if s > 0:
+                add_and_turn(units[s - 1], PRODUCTS)
             if s < SETS:
-                find_top(units[s])
                 subtract_top(units[s])
+                weigh(units[s])
             if s + 2 < SETS:
                 quantise_set(s + 2)
             if s + 1 < SETS:
                 project_gates(units[s + 1])
+                add_offsets(units[s + 1])
+            if s + 3 < SETS:
+                turn_set(s + 3)
             if s < SETS:
-                weigh(units[s])
-            if 0 <= s - 1 < SETS:
-                multiply(units[s - 1])
+                halve_slots(units[s], WEIGHTS, nc.gpsimd)
+            if s > 0:
+                invert(units[s - 1])
+                divide(units[s - 1])
+                rotate(units[s - 1], nc.gpsimd if s < SETS else nc.vector)
             if s < SETS:
-                project_kv(units[s])
-            if 0 <= s - 1 < SETS:
-                add_slots(units[s - 1], nc.gpsimd if s < SETS else nc.vector)
-            if 0 <= s - 2:
-                normalise(units[s - 2])
-                finish(units[s - 2])
-                rotate(units[s - 2], nc.gpsimd if s - 2 < SETS - 1 else nc.vector)
+                add_and_turn(units[s], WEIGHTS)
+                multiply(units[s])
+            if s + 1 < SETS:
+                project_kv(units[s + 1])
+            if s < SETS:
+                halve_slots(units[s], PRODUCTS, nc.vector if last else nc.gpsimd)

@@ -231,17 +231,19 @@ def tile_deepseekv4attention_pa_kernel(
             nc.vector.tensor_max(out=two[:], in0=four[:, 0:2, :], in1=four[:, 2:4, :])
             top = work.tile([P, P], F32, name="top")
             nc.vector.tensor_max(out=top[:], in0=two[:, 0, :], in1=two[:, 1, :])
-            nc.vector.tensor_tensor(
-                out=logit[a][:],
-                in0=logit[a][:],
-                in1=top[:].unsqueeze(1).to_broadcast([P, 2 * SLOTS, P]),
-                op=ALU.subtract,
-            )
+            for half in (LO, HI):
+                nc.vector.tensor_tensor(
+                    out=logit[a][:, slots(half), :],
+                    in0=logit[a][:, slots(half), :],
+                    in1=top[:].unsqueeze(1).to_broadcast([P, SLOTS, P]),
+                    op=ALU.subtract,
+                )
 
         def weigh(a):
             both[a] = work.tile([P, 2, 2 * SLOTS, P], F32, name="both")
             halved[a] = work.tile([P, 2, SLOTS, P], F32, name="halved")
-            nc.scalar.activation(out=both[a][:, WEIGHTS], in_=logit[a][:], func=ACT.Exp)
+            for half in (LO, HI):
+                nc.scalar.activation(out=both[a][:, WEIGHTS, slots(half), :], in_=logit[a][:, slots(half), :], func=ACT.Exp)
 
         def multiply(a):
             if skip(a):

@@ -180,7 +180,7 @@ def tile_deepseekv4attention_pa_kernel(
                 )
             return bank
 
-        gate, kv, logit, both, halved, sums, inverse = {}, {}, {}, {}, {}, {}, {}
+        gate, kv, logit, both, sums, inverse = {}, {}, {}, {}, {}, {}
         pooled_rows = keep.tile([P, SETS, P], F32)
         rotated_rows = keep.tile([P, SETS, P], F32)
         out_rotated = out_0.rearrange("b (p a) f -> p (b a) f", a=SETS)
@@ -241,7 +241,6 @@ def tile_deepseekv4attention_pa_kernel(
 
         def weigh(a):
             both[a] = work.tile([P, 2, 2 * SLOTS, P], F32, name="both")
-            halved[a] = work.tile([P, 2, SLOTS, P], F32, name="halved")
             for half in (LO, HI):
                 nc.scalar.activation(out=both[a][:, WEIGHTS, slots(half), :], in_=logit[a][:, slots(half), :], func=ACT.Exp)
 
@@ -256,17 +255,17 @@ def tile_deepseekv4attention_pa_kernel(
                     op=ALU.mult,
                 )
 
-        def halve_slots(a, which, engine):
-            engine.tensor_tensor(
-                out=halved[a][:, which], in0=both[a][:, which, slots(LO), :], in1=both[a][:, which, slots(HI), :], op=ALU.add
-            )
-
         def add_and_turn(a, which):
             bank = psum_turn.tile([P, PASSES, 2, P], F32, tag="turn", name="sums")
             sums[a, which] = bank[:, 0, 0, :]
-            for s in range(SLOTS):
+            for s in range(2 * SLOTS):
                 nc.tensor.matmul(
-                    out=sums[a, which], lhsT=halved[a][:, which, s, :], rhs=ident[:], start=(s == 0), stop=(s == SLOTS - 1)
+                    out=sums[a, which],
+                    lhsT=both[a][:, which, s, :],
+                    rhs=ident[:],
+                    start=(s == 0),
+                    stop=(s == 2 * SLOTS - 1),
+                    is_transpose=True,
                 )
 
         def invert(a):
@@ -302,7 +301,6 @@ def tile_deepseekv4attention_pa_kernel(
         turn_set(2)
         project_kv(units[0])
         for s in range(SETS + 1):
-            last = s == SETS - 1
             if s > 0:
                 add_and_turn(units[s - 1], PRODUCTS)
             if s < SETS:
@@ -315,8 +313,6 @@ def tile_deepseekv4attention_pa_kernel(
                 add_offsets(units[s + 1])
             if s + 3 < SETS:
                 turn_set(s + 3)
-            if s < SETS:
-                halve_slots(units[s], WEIGHTS, nc.gpsimd)
             if s > 0:
                 invert(units[s - 1])
                 divide(units[s - 1])
@@ -326,5 +322,3 @@ def tile_deepseekv4attention_pa_kernel(
                 multiply(units[s])
             if s + 1 < SETS:
                 project_kv(units[s + 1])
-            if s < SETS:
-                halve_slots(units[s], PRODUCTS, nc.vector if last else nc.gpsimd)

@@ -46,6 +46,8 @@ def tile_deepseekv4attention_pa_kernel(
         psum_kv = stack.enter_context(tc.psum_pool(name="psum_kv", bufs=1))
         stack.enter_context(tc.manual_schedule())
 
+        ape_rows = keep.tile([SLOTS, 2 * P], BF16)
+        nc.sync.dma_start(out=ape_rows[:], in_=ape)
         x = keep.tile([P, SETS * SLOTS, HIDDEN], BF16)
         hidden_rows = hidden.rearrange("b (p i) k -> p (b i) k", i=SETS * SLOTS)
 
@@ -55,6 +57,9 @@ def tile_deepseekv4attention_pa_kernel(
 
         w_words = keep.tile([P, PASSES, 2, 4 * P], U8, align_bytes=64)
         w_scales = keep.tile([P, PASSES, 2, 2 * P], U8, align_bytes=64)
+        warm = keep.tile([P, 2], F32)
+        nc.vector.memset(warm[:], 0.0)
+        nc.scalar.activation(out=warm[:, 0:1], in_=warm[:, 1:2], func=ACT.Sin)
         nc.vector.memset(w_scales[:].bitcast(I32), 0)
 
         def load_weight(which, words, scales):
@@ -82,8 +87,6 @@ def tile_deepseekv4attention_pa_kernel(
         nc.gpsimd.iota(window_int[:], pattern=[[1, SETS]], base=0, channel_multiplier=SETS)
         ident = keep.tile([P, P], F32)
         make_identity(nc, ident[:])
-        ape_rows = keep.tile([SLOTS, 2 * P], BF16)
-        nc.gpsimd.dma_start(out=ape_rows[:], in_=ape)
 
         window = keep.tile([P, SETS], F32)
         nc.vector.tensor_copy(out=window[:], in_=window_int[:])
@@ -120,17 +123,22 @@ def tile_deepseekv4attention_pa_kernel(
         cos_tab = keep.tile([P, SETS, PAIRS, 2], F32)
         sin_tab = keep.tile([P, SETS, PAIRS, 2], F32)
         full_turn = 2.0 * math.pi
-        nc.scalar.activation(out=sin_tab[:, :, :, 0], in_=part[:], func=ACT.Sin, scale=full_turn)
-        nc.scalar.activation(out=sin_tab[:, :, :, 1], in_=part[:], func=ACT.Sin, scale=-full_turn)
-        nc.scalar.activation(out=cos_tab[:, :, :, 0], in_=part_cos[:], func=ACT.Sin, scale=full_turn)
-        nc.scalar.activation(out=cos_tab[:, :, :, 1], in_=part_cos[:], func=ACT.Sin, scale=full_turn)
+
+        def take_sines():
+            nc.scalar.activation(out=sin_tab[:, :, :, 0], in_=part[:], func=ACT.Sin, scale=full_turn)
+            nc.scalar.activation(out=sin_tab[:, :, :, 1], in_=part[:], func=ACT.Sin, scale=-full_turn)
+            nc.scalar.activation(out=cos_tab[:, :, :, 0], in_=part_cos[:], func=ACT.Sin, scale=full_turn)
+            nc.scalar.activation(out=cos_tab[:, :, :, 1], in_=part_cos[:], func=ACT.Sin, scale=full_turn)
+
+        def load_exp_table():
+            nc.scalar.activation(out=warm[:, 0:1], in_=warm[:, 1:2], func=ACT.Exp)
 
         ape_wide = keep.tile([P, 2 * P], F32)
         nc.vector.memset(ape_wide[:], 0.0)
+        nc.vector.tensor_copy(out=ape_wide[0:SLOTS, :], in_=ape_rows[:])
         ape_col = keep.tile([P, 2, SLOTS], F32)
 
         def turn_ape():
-            nc.vector.tensor_copy(out=ape_wide[0:SLOTS, :], in_=ape_rows[:])
             bank = psum_turn.tile([P, PASSES, 2, P], F32, tag="turn")
             for half in (LO, HI):
                 nc.tensor.transpose(bank[:, 0, half, :], ape_wide[:, P * half : P * half + P], ident[:])
@@ -142,21 +150,18 @@ def tile_deepseekv4attention_pa_kernel(
         codes = keep.tile([P, SETS, PASSES, SLOTS * P], U32, align_bytes=64)
         planes = keep.tile([P, SETS, PASSES, SLOTS * P], U8, align_bytes=64)
 
-        def turn_half_set(a, half):
-            for r in (2 * half, 2 * half + 1):
-                bank = psum_turn.tile([P, PASSES, 2, P], F32, tag="turn")
-                for g in range(PASSES):
-                    for u in range(2):
-                        nc.tensor.transpose(
-                            bank[:, g, u, :], x_words[:, SLOTS * a + r, 2 * P * g + u : 2 * P * (g + 1) : 2], ident[:]
-                        )
-                nc.scalar.copy(
-                    out=grouped_words[:, a, :, P * r : P * (r + 1), :], in_=bank[:].rearrange("q g u p -> q g p u")
-                )
+        def turn_tokens(a, r, copy):
+            bank = psum_turn.tile([P, PASSES, 2, P], F32, tag="turn")
+            for g in range(PASSES):
+                for u in range(2):
+                    nc.tensor.transpose(
+                        bank[:, g, u, :], x_words[:, SLOTS * a + r, 2 * P * g + u : 2 * P * (g + 1) : 2], ident[:]
+                    )
+            copy(out=grouped_words[:, a, :, P * r : P * (r + 1), :], in_=bank[:].rearrange("q g u p -> q g p u"))
 
-        def turn_set(a):
-            for half in range(2):
-                turn_half_set(a, half)
+        def turn_shared(a, some_slots):
+            for r in some_slots:
+                turn_tokens(a, r, nc.vector.tensor_copy if r % 2 else nc.scalar.copy)
 
         def quantise_set(a):
             for g in range(PASSES):
@@ -180,7 +185,7 @@ def tile_deepseekv4attention_pa_kernel(
                 )
             return bank
 
-        gate, kv, logit, both, sums, inverse = {}, {}, {}, {}, {}, {}
+        gate, kv, logit, top, both, sums, inverse = {}, {}, {}, {}, {}, {}, {}
         pooled_rows = keep.tile([P, SETS, P], F32)
         rotated_rows = keep.tile([P, SETS, P], F32)
         out_rotated = out_0.rearrange("b (p a) f -> p (b a) f", a=SETS)
@@ -198,11 +203,11 @@ def tile_deepseekv4attention_pa_kernel(
         def slots(half):
             return slice(SLOTS * half, SLOTS * (half + 1))
 
-        def project_gates(a):
-            gate[a] = {
-                LO: project(psum_gate, GATE, LO, (a - 1) % SETS, "gate_lo"),
-                HI: project(psum_gate, GATE, HI, a, "gate_hi"),
-            }
+        def project_gates(a, half):
+            if half == LO:
+                gate[a, LO] = project(psum_gate, GATE, LO, (a - 1) % SETS, "gate_lo")
+            else:
+                gate[a, HI] = project(psum_gate, GATE, HI, a, "gate_hi")
 
         def project_kv(a):
             kv[a] = {
@@ -210,32 +215,34 @@ def tile_deepseekv4attention_pa_kernel(
                 HI: project(psum_kv, KV, HI, a, "kv_hi"),
             }
 
-        def add_offsets(a):
-            logit[a] = work.tile([P, 2 * SLOTS, P], F32, name="logit")
-            if skip(a):
-                nc.gpsimd.memset(logit[a][:, slots(LO), 0:BLOCK], MASKED)
-            for half in (LO, HI):
-                for r in range(SLOTS):
-                    nc.scalar.activation(
-                        out=logit[a][:, SLOTS * half + r, target(a, half)],
-                        in_=gate[a][half][:, r, source(a, half)],
-                        func=ACT.Identity,
-                        bias=ape_col[:, half, r : r + 1],
-                        scale=1.0,
-                    )
+        def add_offsets(a, half):
+            if half == LO:
+                logit[a] = work.tile([P, 2 * SLOTS, P], F32, name="logit")
+                if skip(a):
+                    nc.gpsimd.memset(logit[a][:, slots(LO), 0:BLOCK], MASKED)
+            for r in range(SLOTS):
+                nc.scalar.activation(
+                    out=logit[a][:, SLOTS * half + r, target(a, half)],
+                    in_=gate[a, half][:, r, source(a, half)],
+                    func=ACT.Identity,
+                    bias=ape_col[:, half, r : r + 1],
+                    scale=1.0,
+                )
 
-        def subtract_top(a):
+        def find_top(a):
             four = work.tile([P, 4, P], F32, name="top_four")
             nc.vector.tensor_max(out=four[:], in0=logit[a][:, 0:4, :], in1=logit[a][:, 4:8, :])
             two = work.tile([P, 2, P], F32, name="top_two")
             nc.vector.tensor_max(out=two[:], in0=four[:, 0:2, :], in1=four[:, 2:4, :])
-            top = work.tile([P, P], F32, name="top")
-            nc.vector.tensor_max(out=top[:], in0=two[:, 0, :], in1=two[:, 1, :])
+            top[a] = work.tile([P, P], F32, name="top")
+            nc.vector.tensor_max(out=top[a][:], in0=two[:, 0, :], in1=two[:, 1, :])
+
+        def subtract_top(a):
             for half in (LO, HI):
                 nc.vector.tensor_tensor(
                     out=logit[a][:, slots(half), :],
                     in0=logit[a][:, slots(half), :],
-                    in1=top[:].unsqueeze(1).to_broadcast([P, SLOTS, P]),
+                    in1=top[a][:].unsqueeze(1).to_broadcast([P, SLOTS, P]),
                     op=ALU.subtract,
                 )
 
@@ -289,36 +296,44 @@ def tile_deepseekv4attention_pa_kernel(
             nc.sync.dma_start(out=out_rotated[:, a, :], in_=rotated_rows[:, a, :])
 
         units = [1, 2, 3, 0]
-        turn_set(0)
-        turn_set(1)
-        quantise_set(0)
+        turn_shared(0, range(SLOTS))
+        take_sines()
         turn_ape()
+        quantise_set(0)
+        turn_shared(1, range(SLOTS))
+        load_exp_table()
         quantise_set(1)
-        warm = keep.tile([P, 1], F32)
-        nc.scalar.activation(out=warm[:], in_=freq[:, 0:1], func=ACT.Exp)
-        project_gates(units[0])
-        add_offsets(units[0])
-        turn_set(2)
-        project_kv(units[0])
-        for s in range(SETS + 1):
+        turn_shared(2, (0, 1))
+        project_gates(units[0], LO)
+        add_offsets(units[0], LO)
+        turn_shared(2, (2, 3))
+        project_gates(units[0], HI)
+        add_offsets(units[0], HI)
+        quantise_set(2)
+        for r in range(SLOTS):
+            turn_tokens(3, r, nc.scalar.copy)
+        for s in range(SETS):
+            find_top(units[s])
+            if s + 1 < SETS:
+                project_gates(units[s + 1], LO)
+                add_offsets(units[s + 1], LO)
+                project_gates(units[s + 1], HI)
+            project_kv(units[s])
+            subtract_top(units[s])
+            weigh(units[s])
+            if s + 1 < SETS:
+                add_offsets(units[s + 1], HI)
+            if s == 0:
+                quantise_set(3)
             if s > 0:
                 add_and_turn(units[s - 1], PRODUCTS)
-            if s < SETS:
-                subtract_top(units[s])
-                weigh(units[s])
-            if s + 2 < SETS:
-                quantise_set(s + 2)
-            if s + 1 < SETS:
-                project_gates(units[s + 1])
-                add_offsets(units[s + 1])
-            if s + 3 < SETS:
-                turn_set(s + 3)
-            if s > 0:
                 invert(units[s - 1])
+            multiply(units[s])
+            add_and_turn(units[s], WEIGHTS)
+            if s > 0:
                 divide(units[s - 1])
-                rotate(units[s - 1], nc.gpsimd if s < SETS else nc.vector)
-            if s < SETS:
-                add_and_turn(units[s], WEIGHTS)
-                multiply(units[s])
-            if s + 1 < SETS:
-                project_kv(units[s + 1])
+                rotate(units[s - 1], nc.gpsimd)
+        add_and_turn(units[SETS - 1], PRODUCTS)
+        invert(units[SETS - 1])
+        divide(units[SETS - 1])
+        rotate(units[SETS - 1], nc.vector)

@@ -41,9 +41,9 @@ def tile_deepseekv4attention_pa_kernel(
     with ExitStack() as stack:
         keep = stack.enter_context(tc.tile_pool(name="keep", bufs=1))
         work = stack.enter_context(tc.tile_pool(name="work", bufs=3))
-        psum_turn = stack.enter_context(tc.psum_pool(name="psum_turn", bufs=4))
-        psum_gate = stack.enter_context(tc.psum_pool(name="psum_gate", bufs=1))
-        psum_kv = stack.enter_context(tc.psum_pool(name="psum_kv", bufs=1))
+        psum_turn = stack.enter_context(tc.psum_pool(name="psum_turn", bufs=2))
+        psum_gate = stack.enter_context(tc.psum_pool(name="psum_gate", bufs=2))
+        psum_kv = stack.enter_context(tc.psum_pool(name="psum_kv", bufs=2))
         stack.enter_context(tc.manual_schedule())
 
         ape_rows = keep.tile([SLOTS, 2 * P], BF16)
@@ -138,8 +138,16 @@ def tile_deepseekv4attention_pa_kernel(
         nc.vector.tensor_copy(out=ape_wide[0:SLOTS, :], in_=ape_rows[:])
         ape_col = keep.tile([P, 2, SLOTS], F32)
 
+        banks_taken = []
+
+        def bank_for_transposes():
+            banks_taken.append(1)
+            if len(banks_taken) % 2:
+                return psum_turn.tile([P, PASSES, 2, P], F32, tag="turn", name="turned")
+            return psum_kv.tile([P, PASSES, 2, P], F32, tag="kv", name="turned")
+
         def turn_ape():
-            bank = psum_turn.tile([P, PASSES, 2, P], F32, tag="turn")
+            bank = bank_for_transposes()
             for half in (LO, HI):
                 nc.tensor.transpose(bank[:, 0, half, :], ape_wide[:, P * half : P * half + P], ident[:])
             nc.vector.tensor_copy(out=ape_col[:], in_=bank[:, 0, :, 0:SLOTS])
@@ -151,7 +159,7 @@ def tile_deepseekv4attention_pa_kernel(
         planes = keep.tile([P, SETS, PASSES, SLOTS * P], U8, align_bytes=64)
 
         def turn_tokens(a, r, copy):
-            bank = psum_turn.tile([P, PASSES, 2, P], F32, tag="turn")
+            bank = bank_for_transposes()
             for g in range(PASSES):
                 for u in range(2):
                     nc.tensor.transpose(
@@ -171,8 +179,8 @@ def tile_deepseekv4attention_pa_kernel(
                     in_=grouped[:, a, g].rearrange("q c t -> q (c t)"),
                 )
 
-        def project(pool, which, half, a, name):
-            bank = pool.tile([P, SLOTS, P], F32, name=name)
+        def project(pool, which, half, a, tag):
+            bank = pool.tile([P, SLOTS, P], F32, tag=tag, name="projected")
             for g in range(PASSES):
                 nc.tensor.matmul_mx(
                     out=bank[:].rearrange("f r p -> f (r p)"),
@@ -185,7 +193,7 @@ def tile_deepseekv4attention_pa_kernel(
                 )
             return bank
 
-        gate, kv, logit, top, both, sums, inverse = {}, {}, {}, {}, {}, {}, {}
+        gate, kv, rough, shifted, top, both, sums, inverse = {}, {}, {}, {}, {}, {}, {}, {}
         pooled_rows = keep.tile([P, SETS, P], F32)
         rotated_rows = keep.tile([P, SETS, P], F32)
         out_rotated = out_0.rearrange("b (p a) f -> p (b a) f", a=SETS)
@@ -211,18 +219,20 @@ def tile_deepseekv4attention_pa_kernel(
 
         def project_kv(a):
             kv[a] = {
-                LO: project(psum_kv, KV, LO, (a - 1) % SETS, "kv_lo"),
-                HI: project(psum_kv, KV, HI, a, "kv_hi"),
+                LO: project(psum_kv, KV, LO, (a - 1) % SETS, "kv"),
+                HI: project(psum_kv, KV, HI, a, "kv"),
             }
 
         def add_offsets(a, half):
             if half == LO:
-                logit[a] = work.tile([P, 2 * SLOTS, P], F32, name="logit")
+                rough[a] = work.tile([P, 2 * SLOTS, P], BF16, name="rough")
+                shifted[a] = work.tile([P, 2 * SLOTS, P], F32, name="shifted")
                 if skip(a):
-                    nc.gpsimd.memset(logit[a][:, slots(LO), 0:BLOCK], MASKED)
+                    nc.gpsimd.memset(rough[a][:, slots(LO), 0 : 2 * BLOCK], MASKED)
+                    nc.gpsimd.memset(shifted[a][:, slots(LO), 0:BLOCK], MASKED)
             for r in range(SLOTS):
                 nc.scalar.activation(
-                    out=logit[a][:, SLOTS * half + r, target(a, half)],
+                    out=rough[a][:, SLOTS * half + r, target(a, half)],
                     in_=gate[a, half][:, r, source(a, half)],
                     func=ACT.Identity,
                     bias=ape_col[:, half, r : r + 1],
@@ -230,26 +240,34 @@ def tile_deepseekv4attention_pa_kernel(
                 )
 
         def find_top(a):
-            four = work.tile([P, 4, P], F32, name="top_four")
-            nc.vector.tensor_max(out=four[:], in0=logit[a][:, 0:4, :], in1=logit[a][:, 4:8, :])
-            two = work.tile([P, 2, P], F32, name="top_two")
+            four = work.tile([P, 4, P], BF16, name="top_four")
+            nc.vector.tensor_max(out=four[:], in0=rough[a][:, 0:4, :], in1=rough[a][:, 4:8, :])
+            two = work.tile([P, 2, P], BF16, name="top_two")
             nc.vector.tensor_max(out=two[:], in0=four[:, 0:2, :], in1=four[:, 2:4, :])
-            top[a] = work.tile([P, P], F32, name="top")
+            top[a] = work.tile([P, P], BF16, name="top")
             nc.vector.tensor_max(out=top[a][:], in0=two[:, 0, :], in1=two[:, 1, :])
 
         def subtract_top(a):
             for half in (LO, HI):
+                width = P - skip(a) if half == LO else P
                 nc.vector.tensor_tensor(
-                    out=logit[a][:, slots(half), :],
-                    in0=logit[a][:, slots(half), :],
-                    in1=top[a][:].unsqueeze(1).to_broadcast([P, SLOTS, P]),
+                    out=shifted[a][:, slots(half), target(a, half)],
+                    in0=gate[a, half][:, :, source(a, half)],
+                    in1=top[a][:, target(a, half)].unsqueeze(1).to_broadcast([P, SLOTS, width]),
                     op=ALU.subtract,
                 )
 
         def weigh(a):
             both[a] = work.tile([P, 2, 2 * SLOTS, P], F32, name="both")
             for half in (LO, HI):
-                nc.scalar.activation(out=both[a][:, WEIGHTS, slots(half), :], in_=logit[a][:, slots(half), :], func=ACT.Exp)
+                for r in range(SLOTS):
+                    nc.scalar.activation(
+                        out=both[a][:, WEIGHTS, SLOTS * half + r, :],
+                        in_=shifted[a][:, SLOTS * half + r, :],
+                        func=ACT.Exp,
+                        bias=ape_col[:, half, r : r + 1],
+                        scale=1.0,
+                    )
 
         def multiply(a):
             if skip(a):

@@ -27,6 +27,7 @@ THETA = 10000.0
 KV, GATE = 0, 1
 LO, HI = 0, 1
 WEIGHTS, PRODUCTS = 0, 1
+SIN, COS = 0, 1
 MASKED = -1.0e30
 ROUND_TO_WHOLE = 1.5 * 2.0**23
 BLOCK = 8
@@ -46,50 +47,16 @@ def tile_deepseekv4attention_pa_kernel(
         psum_kv = stack.enter_context(tc.psum_pool(name="psum_kv", bufs=2))
         stack.enter_context(tc.manual_schedule())
 
-        ape_rows = keep.tile([SLOTS, 2 * P], BF16)
-        nc.sync.dma_start(out=ape_rows[:], in_=ape)
-        x = keep.tile([P, SETS * SLOTS, HIDDEN], BF16)
-        hidden_rows = hidden.rearrange("b (p i) k -> p (b i) k", i=SETS * SLOTS)
-
-        def load_half_set(a, half):
-            first = SLOTS * a + 2 * half
-            nc.sync.dma_start(out=x[:, first : first + 2, :], in_=hidden_rows[:, first : first + 2, :])
-
-        w_words = keep.tile([P, PASSES, 2, 4 * P], U8, align_bytes=64)
-        w_scales = keep.tile([P, PASSES, 2, 2 * P], U8, align_bytes=64)
         warm = keep.tile([P, 2], F32)
         nc.vector.memset(warm[:], 0.0)
         nc.scalar.activation(out=warm[:, 0:1], in_=warm[:, 1:2], func=ACT.Sin)
-        nc.vector.memset(w_scales[:].bitcast(I32), 0)
-
-        def load_weight(which, words, scales):
-            nc.sync.dma_start(
-                out=w_words[:, :, which, :].bitcast(I32), in_=words.bitcast(I32).rearrange("g p b -> p g b")
-            )
-            rows = scales.bitcast(I32).rearrange("g q n -> q g n")
-            for quadrant in range(4):
-                nc.sync.dma_start(
-                    out=w_scales[32 * quadrant : 32 * quadrant + 4, :, which, :].bitcast(I32),
-                    in_=rows[4 * quadrant : 4 * quadrant + 4, :, :],
-                )
-
-        for a in (0, 1):
-            for half in range(2):
-                load_half_set(a, half)
-        load_weight(GATE, wgate_words, wgate_scales)
-        for half in range(2):
-            load_half_set(2, half)
-        load_weight(KV, wkv_words, wkv_scales)
-        for half in range(2):
-            load_half_set(3, half)
-
-        window_int = keep.tile([P, SETS], I32)
-        nc.gpsimd.iota(window_int[:], pattern=[[1, SETS]], base=0, channel_multiplier=SETS)
+        window = keep.tile([P, SETS], F32)
+        nc.gpsimd.iota(
+            window[:], pattern=[[1, SETS]], base=0, channel_multiplier=SETS, allow_small_or_imprecise_dtypes=True
+        )
         ident = keep.tile([P, P], F32)
         make_identity(nc, ident[:])
 
-        window = keep.tile([P, SETS], F32)
-        nc.vector.tensor_copy(out=window[:], in_=window_int[:])
         freq = keep.tile([P, PAIRS], F32)
         nc.vector.memset(freq[:, 0:1], 1.0)
         have = 1
@@ -112,26 +79,58 @@ def tile_deepseekv4attention_pa_kernel(
         nc.vector.tensor_scalar(
             out=whole[:], in0=turns[:], scalar1=ROUND_TO_WHOLE, scalar2=ROUND_TO_WHOLE, op0=ALU.add, op1=ALU.subtract
         )
-        part = keep.tile(table, F32)
-        nc.vector.tensor_tensor(out=part[:], in0=turns[:], in1=whole[:], op=ALU.subtract)
+        part = keep.tile([P, 2, SETS, PAIRS], F32)
+        nc.vector.tensor_tensor(out=part[:, SIN], in0=turns[:], in1=whole[:], op=ALU.subtract)
         beyond = keep.tile(table, F32)
-        nc.vector.tensor_scalar(out=beyond[:], in0=part[:], scalar1=0.25, scalar2=None, op0=ALU.is_gt)
-        part_cos = keep.tile(table, F32)
+        nc.vector.tensor_scalar(out=beyond[:], in0=part[:, SIN], scalar1=0.25, scalar2=None, op0=ALU.is_gt)
         nc.vector.scalar_tensor_tensor(
-            out=part_cos[:], in0=part[:], scalar=0.25, in1=beyond[:], op0=ALU.add, op1=ALU.subtract
+            out=part[:, COS], in0=part[:, SIN], scalar=0.25, in1=beyond[:], op0=ALU.add, op1=ALU.subtract
         )
-        cos_tab = keep.tile([P, SETS, PAIRS, 2], F32)
-        sin_tab = keep.tile([P, SETS, PAIRS, 2], F32)
-        full_turn = 2.0 * math.pi
+        trig = keep.tile([P, 2, SETS, PAIRS], F32)
 
         def take_sines():
-            nc.scalar.activation(out=sin_tab[:, :, :, 0], in_=part[:], func=ACT.Sin, scale=full_turn)
-            nc.scalar.activation(out=sin_tab[:, :, :, 1], in_=part[:], func=ACT.Sin, scale=-full_turn)
-            nc.scalar.activation(out=cos_tab[:, :, :, 0], in_=part_cos[:], func=ACT.Sin, scale=full_turn)
-            nc.scalar.activation(out=cos_tab[:, :, :, 1], in_=part_cos[:], func=ACT.Sin, scale=full_turn)
+            nc.scalar.activation(out=trig[:], in_=part[:], func=ACT.Sin, scale=2.0 * math.pi)
 
         def load_exp_table():
             nc.scalar.activation(out=warm[:, 0:1], in_=warm[:, 1:2], func=ACT.Exp)
+
+        ape_rows = keep.tile([SLOTS, 2 * P], BF16)
+        x = keep.tile([P, SETS * SLOTS, HIDDEN], BF16)
+        hidden_rows = hidden.rearrange("b (p i) k -> p (b i) k", i=SETS * SLOTS)
+
+        def load_tokens(first, count):
+            nc.sync.dma_start(out=x[:, first : first + count, :], in_=hidden_rows[:, first : first + count, :])
+
+        def load_half_set(a, half):
+            load_tokens(SLOTS * a + 2 * half, 2)
+
+        w_words = keep.tile([P, PASSES, 2, 4 * P], U8, align_bytes=64)
+        w_scales = keep.tile([P, PASSES, 2, 2 * P], U8, align_bytes=64)
+        nc.vector.memset(w_scales[:].bitcast(I32), 0)
+
+        def load_weight(which, words, scales):
+            nc.sync.dma_start(
+                out=w_words[:, :, which, :].bitcast(I32), in_=words.bitcast(I32).rearrange("g p b -> p g b")
+            )
+            rows = scales.bitcast(I32).rearrange("g q n -> q g n")
+            for quadrant in range(4):
+                nc.sync.dma_start(
+                    out=w_scales[32 * quadrant : 32 * quadrant + 4, :, which, :].bitcast(I32),
+                    in_=rows[4 * quadrant : 4 * quadrant + 4, :, :],
+                )
+
+        load_tokens(0, 1)
+        load_tokens(1, 1)
+        nc.sync.dma_start(out=ape_rows[:], in_=ape)
+        load_half_set(0, 1)
+        for half in range(2):
+            load_half_set(1, half)
+        load_weight(GATE, wgate_words, wgate_scales)
+        for half in range(2):
+            load_half_set(2, half)
+        load_weight(KV, wkv_words, wkv_scales)
+        for half in range(2):
+            load_half_set(3, half)
 
         ape_wide = keep.tile([P, 2 * P], F32)
         nc.vector.memset(ape_wide[:], 0.0)
@@ -306,11 +305,12 @@ def tile_deepseekv4attention_pa_kernel(
             by_cos = work.tile([P, PAIRS, 2], F32, name="by_cos")
             by_sin = work.tile([P, PAIRS, 2], F32, name="by_sin")
             tail = pooled_rows[:, a, P - ROPE : P].rearrange("p (j e) -> p j e", e=2)
-            engine.tensor_tensor(out=by_cos[:], in0=tail, in1=cos_tab[:, a, :, :], op=ALU.mult)
-            engine.tensor_tensor(out=by_sin[:], in0=tail, in1=sin_tab[:, a, :, :], op=ALU.mult)
-            turned = rotated_rows[:, a, P - ROPE : P].rearrange("p (j e) -> p j e", e=2)
-            for e in range(2):
-                engine.tensor_tensor(out=turned[:, :, e], in0=by_cos[:, :, e], in1=by_sin[:, :, 1 - e], op=ALU.add)
+            pair = [P, PAIRS, 2]
+            engine.tensor_tensor(out=by_cos[:], in0=tail, in1=trig[:, COS, a, :].unsqueeze(2).to_broadcast(pair), op=ALU.mult)
+            engine.tensor_tensor(out=by_sin[:], in0=tail, in1=trig[:, SIN, a, :].unsqueeze(2).to_broadcast(pair), op=ALU.mult)
+            spun = rotated_rows[:, a, P - ROPE : P].rearrange("p (j e) -> p j e", e=2)
+            engine.tensor_tensor(out=spun[:, :, 0], in0=by_cos[:, :, 0], in1=by_sin[:, :, 1], op=ALU.subtract)
+            engine.tensor_tensor(out=spun[:, :, 1], in0=by_cos[:, :, 1], in1=by_sin[:, :, 0], op=ALU.add)
             nc.sync.dma_start(out=out_rotated[:, a, :], in_=rotated_rows[:, a, :])
 
         units = [1, 2, 3, 0]

@@ -168,7 +168,8 @@ def tile_deepseekv4attention_pa_kernel(
 
         def turn_shared(a, some_slots):
             for r in some_slots:
-                turn_tokens(a, r, nc.vector.tensor_copy if r % 2 else nc.scalar.copy)
+                vectors = r == SLOTS - 1 or (a == 0 and r == 1)
+                turn_tokens(a, r, nc.vector.tensor_copy if vectors else nc.scalar.copy)
 
         def quantise_set(a):
             for g in range(PASSES):

@@ -94,6 +94,11 @@ def tile_deepseekv4attention_pa_kernel(
         def load_exp_table():
             nc.scalar.activation(out=warm[:, 0:1], in_=warm[:, 1:2], func=ACT.Exp)
 
+        rough_skip = keep.tile([P, 2 * SLOTS, P], BF16)
+        shifted_skip = keep.tile([P, 2 * SLOTS, P], F32)
+        nc.gpsimd.memset(rough_skip[:, 0:SLOTS, 0 : 2 * BLOCK], MASKED)
+        nc.gpsimd.memset(shifted_skip[:, 0:SLOTS, 0:BLOCK], MASKED)
+
         ape_rows = keep.tile([SLOTS, 2 * P], BF16)
         x = keep.tile([P, SETS * SLOTS, HIDDEN], BF16)
         hidden_rows = hidden.rearrange("b (p i) k -> p (b i) k", i=SETS * SLOTS)
@@ -225,11 +230,11 @@ def tile_deepseekv4attention_pa_kernel(
 
         def add_offsets(a, half):
             if half == LO:
-                rough[a] = work.tile([P, 2 * SLOTS, P], BF16, name="rough")
-                shifted[a] = work.tile([P, 2 * SLOTS, P], F32, name="shifted")
                 if skip(a):
-                    nc.gpsimd.memset(rough[a][:, slots(LO), 0 : 2 * BLOCK], MASKED)
-                    nc.gpsimd.memset(shifted[a][:, slots(LO), 0:BLOCK], MASKED)
+                    rough[a], shifted[a] = rough_skip, shifted_skip
+                else:
+                    rough[a] = work.tile([P, 2 * SLOTS, P], BF16, name="rough")
+                    shifted[a] = work.tile([P, 2 * SLOTS, P], F32, name="shifted")
             for r in range(SLOTS):
                 nc.scalar.activation(
                     out=rough[a][:, SLOTS * half + r, target(a, half)],

@@ -109,18 +109,19 @@ def tile_deepseekv4attention_pa_kernel(
         def load_half_set(a, half):
             load_tokens(SLOTS * a + 2 * half, 2)
 
-        w_words = keep.tile([P, PASSES, 2, 4 * P], U8, align_bytes=64)
-        w_scales = keep.tile([P, PASSES, 2, 2 * P], U8, align_bytes=64)
-        nc.vector.memset(w_scales[:].bitcast(I32), 0)
+        w_words = [keep.tile([P, PASSES, 4 * P], U8, align_bytes=64, name="words_%d" % which) for which in (KV, GATE)]
+        w_scales = [keep.tile([P, PASSES, 2 * P], U8, align_bytes=64, name="scales_%d" % which) for which in (KV, GATE)]
+        for which in (GATE, KV):
+            nc.gpsimd.memset(w_scales[which][:].bitcast(I32), 0)
 
         def load_weight(which, words, scales):
             nc.sync.dma_start(
-                out=w_words[:, :, which, :].bitcast(I32), in_=words.bitcast(I32).rearrange("g p b -> p g b")
+                out=w_words[which][:].bitcast(I32), in_=words.bitcast(I32).rearrange("g p b -> p g b")
             )
             rows = scales.bitcast(I32).rearrange("g q n -> q g n")
             for quadrant in range(4):
                 nc.sync.dma_start(
-                    out=w_scales[32 * quadrant : 32 * quadrant + 4, :, which, :].bitcast(I32),
+                    out=w_scales[which][32 * quadrant : 32 * quadrant + 4, :, :].bitcast(I32),
                     in_=rows[4 * quadrant : 4 * quadrant + 4, :, :],
                 )
 
@@ -133,9 +134,9 @@ def tile_deepseekv4attention_pa_kernel(
         load_weight(GATE, wgate_words, wgate_scales)
         for half in range(2):
             load_half_set(2, half)
-        load_weight(KV, wkv_words, wkv_scales)
         for half in range(2):
             load_half_set(3, half)
+        load_weight(KV, wkv_words, wkv_scales)
 
         ape_wide = keep.tile([P, 2 * P], F32)
         nc.vector.memset(ape_wide[:], 0.0)
@@ -189,8 +190,8 @@ def tile_deepseekv4attention_pa_kernel(
             for g in range(PASSES):
                 nc.tensor.matmul_mx(
                     out=bank[:].rearrange("f r p -> f (r p)"),
-                    lhsT=w_words[:, g, which, 2 * P * half : 2 * P * (half + 1)].bitcast(FP4X4),
-                    lhsT_scale=w_scales[:, g, which, P * half : P * (half + 1)],
+                    lhsT=w_words[which][:, g, 2 * P * half : 2 * P * (half + 1)].bitcast(FP4X4),
+                    lhsT_scale=w_scales[which][:, g, P * half : P * (half + 1)],
                     rhs=codes[:, a, g, :].bitcast(FP8X4),
                     rhs_scale=planes[:, a, g, :],
                     start=(g == 0),

@@ -172,17 +172,13 @@ def tile_deepseekv4attention_pa_kernel(
                     )
             copy(out=grouped_words[:, a, :, P * r : P * (r + 1), :], in_=bank[:].rearrange("q g u p -> q g p u"))
 
-        def turn_shared(a, some_slots):
-            for r in some_slots:
-                vectors = r == SLOTS - 1 or (a == 0 and r == 1)
-                turn_tokens(a, r, nc.vector.tensor_copy if vectors else nc.scalar.copy)
-
-        def quantise_set(a):
+        def quantise(a, first=0, count=SLOTS):
+            columns = slice(P * first, P * (first + count))
             for g in range(PASSES):
                 nc.vector.quantize_mx(
-                    out=codes[:, a, g, :].bitcast(FP8X4),
-                    scales=planes[:, a, g, :],
-                    in_=grouped[:, a, g].rearrange("q c t -> q (c t)"),
+                    out=codes[:, a, g, columns].bitcast(FP8X4),
+                    scales=planes[:, a, g, columns],
+                    in_=grouped[:, a, g, columns, :].rearrange("q c t -> q (c t)"),
                 )
 
         def project(pool, which, half, a, tag):
@@ -199,7 +195,7 @@ def tile_deepseekv4attention_pa_kernel(
                 )
             return bank
 
-        gate, kv, rough, shifted, top, both, sums, inverse = {}, {}, {}, {}, {}, {}, {}, {}
+        gate, kv, rough, shifted, four, two, top, both, sums, inverse = {}, {}, {}, {}, {}, {}, {}, {}, {}, {}
         pooled_rows = keep.tile([P, SETS, P], F32)
         rotated_rows = keep.tile([P, SETS, P], F32)
         out_rotated = out_0.rearrange("b (p a) f -> p (b a) f", a=SETS)
@@ -245,13 +241,17 @@ def tile_deepseekv4attention_pa_kernel(
                     scale=1.0,
                 )
 
-        def find_top(a):
-            four = work.tile([P, 4, P], BF16, name="top_four")
-            nc.vector.tensor_max(out=four[:], in0=rough[a][:, 0:4, :], in1=rough[a][:, 4:8, :])
-            two = work.tile([P, 2, P], BF16, name="top_two")
-            nc.vector.tensor_max(out=two[:], in0=four[:, 0:2, :], in1=four[:, 2:4, :])
+        def max_four(a):
+            four[a] = work.tile([P, 4, P], BF16, name="four")
+            nc.vector.tensor_max(out=four[a][:], in0=rough[a][:, 0:4, :], in1=rough[a][:, 4:8, :])
+
+        def max_two(a):
+            two[a] = work.tile([P, 2, P], BF16, name="two")
+            nc.vector.tensor_max(out=two[a][:], in0=four[a][:, 0:2, :], in1=four[a][:, 2:4, :])
+
+        def max_one(a):
             top[a] = work.tile([P, P], BF16, name="top")
-            nc.vector.tensor_max(out=top[a][:], in0=two[:, 0, :], in1=two[:, 1, :])
+            nc.vector.tensor_max(out=top[a][:], in0=two[a][:, 0, :], in1=two[a][:, 1, :])
 
         def subtract_top(a):
             for half in (LO, HI):
@@ -275,20 +275,22 @@ def tile_deepseekv4attention_pa_kernel(
                         scale=1.0,
                     )
 
-        def multiply(a):
-            if skip(a):
+        def multiply(a, half):
+            if skip(a) and half == LO:
                 nc.vector.memset(both[a][:, PRODUCTS, slots(LO), 0 : skip(a)], 0.0)
-            for half in (LO, HI):
-                nc.vector.tensor_tensor(
-                    out=both[a][:, PRODUCTS, slots(half), target(a, half)],
-                    in0=kv[a][half][:, :, source(a, half)],
-                    in1=both[a][:, WEIGHTS, slots(half), target(a, half)],
-                    op=ALU.mult,
-                )
+            nc.vector.tensor_tensor(
+                out=both[a][:, PRODUCTS, slots(half), target(a, half)],
+                in0=kv[a][half][:, :, source(a, half)],
+                in1=both[a][:, WEIGHTS, slots(half), target(a, half)],
+                op=ALU.mult,
+            )
 
         def add_and_turn(a, which):
-            bank = psum_turn.tile([P, PASSES, 2, P], F32, tag="turn", name="sums")
-            sums[a, which] = bank[:, 0, 0, :]
+            if a == 0 and which == PRODUCTS:
+                bank = psum_gate.tile([P, SLOTS, P], F32, tag="gate_lo", name="sums")
+            else:
+                bank = psum_turn.tile([P, SLOTS, P], F32, tag="turn", name="sums")
+            sums[a, which] = bank[:, 0, :]
             for s in range(2 * SLOTS):
                 nc.tensor.matmul(
                     out=sums[a, which],
@@ -321,44 +323,69 @@ def tile_deepseekv4attention_pa_kernel(
             nc.sync.dma_start(out=out_rotated[:, a, :], in_=rotated_rows[:, a, :])
 
         units = [1, 2, 3, 0]
-        turn_shared(0, range(SLOTS))
+        V, S = nc.vector.tensor_copy, nc.scalar.copy
+        turn_tokens(0, 0, S)
+        turn_tokens(0, 1, V)
+        turn_tokens(0, 2, S)
+        turn_tokens(0, 3, V)
         take_sines()
-        turn_ape()
-        quantise_set(0)
-        turn_shared(1, range(SLOTS))
         load_exp_table()
-        quantise_set(1)
-        turn_shared(2, (0, 1))
-        project_gates(units[0], LO)
-        add_offsets(units[0], LO)
-        turn_shared(2, (2, 3))
-        project_gates(units[0], HI)
-        add_offsets(units[0], HI)
-        quantise_set(2)
+        turn_ape()
+        quantise(0)
+        turn_tokens(1, 0, S)
+        turn_tokens(1, 1, S)
+        turn_tokens(1, 2, S)
+        turn_tokens(1, 3, V)
+        quantise(1)
+        project_gates(1, LO)
+        add_offsets(1, LO)
+        turn_tokens(2, 0, V)
+        turn_tokens(2, 1, S)
+        turn_tokens(2, 2, S)
+        turn_tokens(2, 3, V)
+        project_gates(1, HI)
+        add_offsets(1, HI)
+        quantise(2)
         for r in range(SLOTS):
-            turn_tokens(3, r, nc.scalar.copy)
+            turn_tokens(3, r, V if r == 0 else S)
+        project_gates(2, LO)
+        add_offsets(2, LO)
+        project_gates(2, HI)
+        add_offsets(2, HI)
+        project_kv(1)
+        max_four(1)
+        max_two(1)
+        max_one(1)
         for s in range(SETS):
-            find_top(units[s])
-            if s + 1 < SETS:
-                project_gates(units[s + 1], LO)
-                add_offsets(units[s + 1], LO)
-                project_gates(units[s + 1], HI)
-            project_kv(units[s])
-            subtract_top(units[s])
-            weigh(units[s])
-            if s + 1 < SETS:
-                add_offsets(units[s + 1], HI)
+            a = units[s]
+            subtract_top(a)
             if s == 0:
-                quantise_set(3)
+                quantise(3)
+            if s + 2 < SETS:
+                project_gates(units[s + 2], LO)
+                project_gates(units[s + 2], HI)
+            weigh(a)
             if s > 0:
-                add_and_turn(units[s - 1], PRODUCTS)
                 invert(units[s - 1])
-            multiply(units[s])
-            add_and_turn(units[s], WEIGHTS)
+            if s + 2 < SETS:
+                add_offsets(units[s + 2], LO)
+                add_offsets(units[s + 2], HI)
+            if s + 1 < SETS:
+                max_four(units[s + 1])
+            multiply(a, LO)
+            if s + 1 < SETS:
+                max_two(units[s + 1])
+            multiply(a, HI)
+            add_and_turn(a, WEIGHTS)
+            if s + 1 < SETS:
+                project_kv(units[s + 1])
+            add_and_turn(a, PRODUCTS)
             if s > 0:
                 divide(units[s - 1])
+            if s > 0:
                 rotate(units[s - 1], nc.gpsimd)
-        add_and_turn(units[SETS - 1], PRODUCTS)
+            if s + 1 < SETS:
+                max_one(units[s + 1])
         invert(units[SETS - 1])
         divide(units[SETS - 1])
         rotate(units[SETS - 1], nc.vector)

@@ -32,6 +32,8 @@ MASKED = -1.0e30
 ROUND_TO_WHOLE = 1.5 * 2.0**23
 BLOCK = 8
 
+LAST = 0
+
 FLOPS = 2 * TOKENS * HIDDEN * 4 * P
 
 
@@ -103,11 +105,8 @@ def tile_deepseekv4attention_pa_kernel(
         x = keep.tile([P, SETS * SLOTS, HIDDEN], BF16)
         hidden_rows = hidden.rearrange("b (p i) k -> p (b i) k", i=SETS * SLOTS)
 
-        def load_tokens(first, count):
-            nc.sync.dma_start(out=x[:, first : first + count, :], in_=hidden_rows[:, first : first + count, :])
-
-        def load_half_set(a, half):
-            load_tokens(SLOTS * a + 2 * half, 2)
+        def load_tokens(i):
+            nc.sync.dma_start(out=x[:, i, :], in_=hidden_rows[:, i, :])
 
         w_words = [keep.tile([P, PASSES, 4 * P], U8, align_bytes=64, name="words_%d" % which) for which in (KV, GATE)]
         w_scales = [keep.tile([P, PASSES, 2 * P], U8, align_bytes=64, name="scales_%d" % which) for which in (KV, GATE)]
@@ -125,17 +124,14 @@ def tile_deepseekv4attention_pa_kernel(
                     in_=rows[4 * quadrant : 4 * quadrant + 4, :, :],
                 )
 
-        load_tokens(0, 1)
-        load_tokens(1, 1)
+        for i in range(2):
+            load_tokens(i)
         nc.sync.dma_start(out=ape_rows[:], in_=ape)
-        load_half_set(0, 1)
-        for half in range(2):
-            load_half_set(1, half)
+        for i in range(2, 2 * SLOTS):
+            load_tokens(i)
         load_weight(GATE, wgate_words, wgate_scales)
-        for half in range(2):
-            load_half_set(2, half)
-        for half in range(2):
-            load_half_set(3, half)
+        for i in range(2 * SLOTS, SETS * SLOTS):
+            load_tokens(i)
         load_weight(KV, wkv_words, wkv_scales)
 
         ape_wide = keep.tile([P, 2 * P], F32)
@@ -220,10 +216,9 @@ def tile_deepseekv4attention_pa_kernel(
                 gate[a, HI] = project(psum_gate, GATE, HI, a, "gate_hi")
 
         def project_kv(a):
-            kv[a] = {
-                LO: project(psum_kv, KV, LO, (a - 1) % SETS, "kv"),
-                HI: project(psum_kv, KV, HI, a, "kv"),
-            }
+            for half in (LO, HI):
+                pool, tag = (psum_gate, ("gate_lo", "gate_hi")[half]) if a == LAST else (psum_kv, "kv")
+                kv[a, half] = project(pool, KV, half, (a - 1) % SETS if half == LO else a, tag)
 
         def add_offsets(a, half):
             if half == LO:
@@ -253,41 +248,44 @@ def tile_deepseekv4attention_pa_kernel(
             top[a] = work.tile([P, P], BF16, name="top")
             nc.vector.tensor_max(out=top[a][:], in0=two[a][:, 0, :], in1=two[a][:, 1, :])
 
-        def subtract_top(a):
+        def subtract_top(a, step=SLOTS):
             for half in (LO, HI):
                 width = P - skip(a) if half == LO else P
-                nc.vector.tensor_tensor(
-                    out=shifted[a][:, slots(half), target(a, half)],
-                    in0=gate[a, half][:, :, source(a, half)],
-                    in1=top[a][:, target(a, half)].unsqueeze(1).to_broadcast([P, SLOTS, width]),
-                    op=ALU.subtract,
-                )
-
-        def weigh(a):
-            both[a] = work.tile([P, 2, 2 * SLOTS, P], F32, name="both")
-            for half in (LO, HI):
-                for r in range(SLOTS):
-                    nc.scalar.activation(
-                        out=both[a][:, WEIGHTS, SLOTS * half + r, :],
-                        in_=shifted[a][:, SLOTS * half + r, :],
-                        func=ACT.Exp,
-                        bias=ape_col[:, half, r : r + 1],
-                        scale=1.0,
+                for r in range(0, SLOTS, step):
+                    nc.vector.tensor_tensor(
+                        out=shifted[a][:, SLOTS * half + r : SLOTS * half + r + step, target(a, half)],
+                        in0=gate[a, half][:, r : r + step, source(a, half)],
+                        in1=top[a][:, target(a, half)].unsqueeze(1).to_broadcast([P, step, width]),
+                        op=ALU.subtract,
                     )
 
-        def multiply(a, half):
+        def weigh(a, half):
+            if half == LO:
+                both[a] = work.tile([P, 2, 2 * SLOTS, P], F32, name="both")
+            for r in range(SLOTS):
+                nc.scalar.activation(
+                    out=both[a][:, WEIGHTS, SLOTS * half + r, :],
+                    in_=shifted[a][:, SLOTS * half + r, :],
+                    func=ACT.Exp,
+                    bias=ape_col[:, half, r : r + 1],
+                    scale=1.0,
+                )
+
+        def multiply(a, half, step=SLOTS):
             if skip(a) and half == LO:
                 nc.vector.memset(both[a][:, PRODUCTS, slots(LO), 0 : skip(a)], 0.0)
-            nc.vector.tensor_tensor(
-                out=both[a][:, PRODUCTS, slots(half), target(a, half)],
-                in0=kv[a][half][:, :, source(a, half)],
-                in1=both[a][:, WEIGHTS, slots(half), target(a, half)],
-                op=ALU.mult,
-            )
+            for r in range(0, SLOTS, step):
+                some = slice(SLOTS * half + r, SLOTS * half + r + step)
+                nc.vector.tensor_tensor(
+                    out=both[a][:, PRODUCTS, some, target(a, half)],
+                    in0=kv[a, half][:, r : r + step, source(a, half)],
+                    in1=both[a][:, WEIGHTS, some, target(a, half)],
+                    op=ALU.mult,
+                )
 
         def add_and_turn(a, which):
-            if a == 0 and which == PRODUCTS:
-                bank = psum_gate.tile([P, SLOTS, P], F32, tag="gate_lo", name="sums")
+            if a == LAST:
+                bank = psum_kv.tile([P, SLOTS, P], F32, tag="kv", name="sums")
             else:
                 bank = psum_turn.tile([P, SLOTS, P], F32, tag="turn", name="sums")
             sums[a, which] = bank[:, 0, :]
@@ -320,6 +318,8 @@ def tile_deepseekv4attention_pa_kernel(
             spun = rotated_rows[:, a, P - ROPE : P].rearrange("p (j e) -> p j e", e=2)
             engine.tensor_tensor(out=spun[:, :, 0], in0=by_cos[:, :, 0], in1=by_sin[:, :, 1], op=ALU.subtract)
             engine.tensor_tensor(out=spun[:, :, 1], in0=by_cos[:, :, 1], in1=by_sin[:, :, 0], op=ALU.add)
+
+        def store_rotated(a):
             nc.sync.dma_start(out=out_rotated[:, a, :], in_=rotated_rows[:, a, :])
 
         units = [1, 2, 3, 0]
@@ -339,53 +339,73 @@ def tile_deepseekv4attention_pa_kernel(
         quantise(1)
         project_gates(1, LO)
         add_offsets(1, LO)
-        turn_tokens(2, 0, V)
+        turn_tokens(2, 0, S)
         turn_tokens(2, 1, S)
         turn_tokens(2, 2, S)
         turn_tokens(2, 3, V)
         project_gates(1, HI)
         add_offsets(1, HI)
         quantise(2)
-        for r in range(SLOTS):
-            turn_tokens(3, r, V if r == 0 else S)
+        turn_tokens(3, 0, V)
+        turn_tokens(3, 1, S)
+        turn_tokens(3, 2, S)
+        turn_tokens(3, 3, S)
         project_gates(2, LO)
         add_offsets(2, LO)
         project_gates(2, HI)
-        add_offsets(2, HI)
         project_kv(1)
         max_four(1)
         max_two(1)
         max_one(1)
-        for s in range(SETS):
-            a = units[s]
-            subtract_top(a)
-            if s == 0:
-                quantise(3)
+        subtract_top(1)
+        weigh(1, LO)
+        add_offsets(2, HI)
+        weigh(1, HI)
+        quantise(3)
+        multiply(1, LO)
+        max_four(2)
+        max_two(2)
+        multiply(1, HI)
+        project_gates(3, LO)
+        project_gates(3, HI)
+        add_offsets(3, LO)
+        add_offsets(3, HI)
+        add_and_turn(1, WEIGHTS)
+        project_kv(2)
+        add_and_turn(1, PRODUCTS)
+        max_one(2)
+        for s in range(1, SETS):
+            a, before = units[s], units[s - 1]
+            subtract_top(a, SLOTS if s + 1 < SETS else 4)
             if s + 2 < SETS:
                 project_gates(units[s + 2], LO)
                 project_gates(units[s + 2], HI)
-            weigh(a)
-            if s > 0:
-                invert(units[s - 1])
+            elif s + 1 < SETS:
+                project_kv(LAST)
+            weigh(a, LO)
+            weigh(a, HI)
+            invert(before)
             if s + 2 < SETS:
                 add_offsets(units[s + 2], LO)
                 add_offsets(units[s + 2], HI)
             if s + 1 < SETS:
                 max_four(units[s + 1])
-            multiply(a, LO)
+            multiply(a, LO, SLOTS if s + 1 < SETS else 2)
             if s + 1 < SETS:
                 max_two(units[s + 1])
-            multiply(a, HI)
+            multiply(a, HI, SLOTS if s + 1 < SETS else 2)
             add_and_turn(a, WEIGHTS)
-            if s + 1 < SETS:
+            if s + 2 < SETS:
                 project_kv(units[s + 1])
             add_and_turn(a, PRODUCTS)
-            if s > 0:
-                divide(units[s - 1])
-            if s > 0:
-                rotate(units[s - 1], nc.gpsimd)
             if s + 1 < SETS:
                 max_one(units[s + 1])
-        invert(units[SETS - 1])
-        divide(units[SETS - 1])
-        rotate(units[SETS - 1], nc.vector)
+            divide(before)
+            rotate(before, nc.gpsimd)
+            if s + 1 < SETS:
+                store_rotated(before)
+        invert(LAST)
+        divide(LAST)
+        store_rotated(units[SETS - 2])
+        rotate(LAST, nc.vector)
+        store_rotated(LAST)

@@ -98,6 +98,8 @@ def tile_deepseekv4attention_pa_kernel(
 
         rough_skip = keep.tile([P, 2 * SLOTS, P], BF16)
         shifted_skip = keep.tile([P, 2 * SLOTS, P], F32)
+        both_skip = keep.tile([P, 2, 2 * SLOTS, P], F32)
+        nc.gpsimd.memset(both_skip[:, PRODUCTS, 0:SLOTS, 0:BLOCK], 0.0)
         nc.gpsimd.memset(rough_skip[:, 0:SLOTS, 0 : 2 * BLOCK], MASKED)
         nc.gpsimd.memset(shifted_skip[:, 0:SLOTS, 0:BLOCK], MASKED)
 
@@ -192,6 +194,7 @@ def tile_deepseekv4attention_pa_kernel(
             return bank
 
         gate, kv, rough, shifted, four, two, top, both, sums, inverse = {}, {}, {}, {}, {}, {}, {}, {}, {}, {}
+        weights, joined = {}, {}
         pooled_rows = keep.tile([P, SETS, P], F32)
         rotated_rows = keep.tile([P, SETS, P], F32)
         out_rotated = out_0.rearrange("b (p a) f -> p (b a) f", a=SETS)
@@ -261,7 +264,7 @@ def tile_deepseekv4attention_pa_kernel(
 
         def weigh(a, half):
             if half == LO:
-                both[a] = work.tile([P, 2, 2 * SLOTS, P], F32, name="both")
+                both[a] = both_skip if skip(a) else work.tile([P, 2, 2 * SLOTS, P], F32, name="both")
             for r in range(SLOTS):
                 nc.scalar.activation(
                     out=both[a][:, WEIGHTS, SLOTS * half + r, :],
@@ -272,8 +275,6 @@ def tile_deepseekv4attention_pa_kernel(
                 )
 
         def multiply(a, half, step=SLOTS):
-            if skip(a) and half == LO:
-                nc.vector.memset(both[a][:, PRODUCTS, slots(LO), 0 : skip(a)], 0.0)
             for r in range(0, SLOTS, step):
                 some = slice(SLOTS * half + r, SLOTS * half + r + step)
                 nc.vector.tensor_tensor(
@@ -299,12 +300,29 @@ def tile_deepseekv4attention_pa_kernel(
                     is_transpose=True,
                 )
 
+        def fetch_weights(a):
+            weights[a] = work.tile([P, 2, P // 2], F32, name="weights")
+            nc.scalar.copy(out=weights[a][:].rearrange("p h f -> p (h f)"), in_=sums[a, WEIGHTS])
+            joined[a] = work.tile([P, P // 2], F32, name="joined")
+            nc.gpsimd.tensor_tensor(out=joined[a][:], in0=weights[a][:, 0], in1=weights[a][:, 1], op=ALU.mult)
+
+        def invert_joined(a):
+            shared = work.tile([P, P // 2], F32, name="shared")
+            nc.vector.reciprocal(out=shared[:], in_=joined[a][:])
+            inverse[a] = work.tile([P, 2, P // 2], F32, name="inverse")
+            nc.gpsimd.tensor_tensor(
+                out=inverse[a][:],
+                in0=weights[a][:, ::-1, :],
+                in1=shared[:].unsqueeze(1).to_broadcast([P, 2, P // 2]),
+                op=ALU.mult,
+            )
+
         def invert(a):
-            inverse[a] = work.tile([P, P], F32, name="inverse")
-            nc.vector.reciprocal(out=inverse[a][:], in_=sums[a, WEIGHTS])
+            inverse[a] = work.tile([P, 2, P // 2], F32, name="inverse")
+            nc.vector.reciprocal(out=inverse[a][:].rearrange("p h f -> p (h f)"), in_=sums[a, WEIGHTS])
 
         def divide(a):
-            nc.vector.tensor_tensor(out=pooled_rows[:, a, :], in0=sums[a, PRODUCTS], in1=inverse[a][:], op=ALU.mult)
+            nc.vector.tensor_tensor(out=pooled_rows[:, a, :], in0=sums[a, PRODUCTS], in1=inverse[a][:].rearrange("p h f -> p (h f)"), op=ALU.mult)
             nc.sync.dma_start(out=out_pooled[:, a, :], in_=pooled_rows[:, a, :])
 
         def rotate(a, engine):
@@ -368,9 +386,10 @@ def tile_deepseekv4attention_pa_kernel(
         multiply(1, HI)
         project_gates(3, LO)
         project_gates(3, HI)
-        add_offsets(3, LO)
-        add_offsets(3, HI)
         add_and_turn(1, WEIGHTS)
+        add_offsets(3, LO)
+        fetch_weights(1)
+        add_offsets(3, HI)
         project_kv(2)
         add_and_turn(1, PRODUCTS)
         max_one(2)
@@ -384,7 +403,11 @@ def tile_deepseekv4attention_pa_kernel(
                 project_kv(LAST)
             weigh(a, LO)
             weigh(a, HI)
-            invert(before)
+            if before == units[0]:
+                invert_joined(before)
+            else:
+                invert(before)
+            add_and_turn(a, WEIGHTS)
             if s + 2 < SETS:
                 add_offsets(units[s + 2], LO)
                 add_offsets(units[s + 2], HI)
@@ -393,16 +416,18 @@ def tile_deepseekv4attention_pa_kernel(
             multiply(a, LO, SLOTS if s + 1 < SETS else 2)
             if s + 1 < SETS:
                 max_two(units[s + 1])
+            if s + 1 == SETS:
+                divide(before)
+                rotate(before, nc.gpsimd)
             multiply(a, HI, SLOTS if s + 1 < SETS else 2)
-            add_and_turn(a, WEIGHTS)
             if s + 2 < SETS:
                 project_kv(units[s + 1])
             add_and_turn(a, PRODUCTS)
             if s + 1 < SETS:
                 max_one(units[s + 1])
-            divide(before)
-            rotate(before, nc.gpsimd)
             if s + 1 < SETS:
+                divide(before)
+                rotate(before, nc.gpsimd)
                 store_rotated(before)
         invert(LAST)
         divide(LAST)

@@ -27,7 +27,7 @@ THETA = 10000.0
 KV, GATE = 0, 1
 LO, HI = 0, 1
 WEIGHTS, PRODUCTS = 0, 1
-SIN, COS = 0, 1
+MINUS_SIN, SIN, COS = 0, 1, 2
 MASKED = -1.0e30
 ROUND_TO_WHOLE = 1.5 * 2.0**23
 BLOCK = 8
@@ -81,14 +81,15 @@ def tile_deepseekv4attention_pa_kernel(
         nc.vector.tensor_scalar(
             out=whole[:], in0=turns[:], scalar1=ROUND_TO_WHOLE, scalar2=ROUND_TO_WHOLE, op0=ALU.add, op1=ALU.subtract
         )
-        part = keep.tile([P, 2, SETS, PAIRS], F32)
+        part = keep.tile([P, 3, SETS, PAIRS], F32)
         nc.vector.tensor_tensor(out=part[:, SIN], in0=turns[:], in1=whole[:], op=ALU.subtract)
+        nc.vector.tensor_tensor(out=part[:, MINUS_SIN], in0=whole[:], in1=turns[:], op=ALU.subtract)
         beyond = keep.tile(table, F32)
         nc.vector.tensor_scalar(out=beyond[:], in0=part[:, SIN], scalar1=0.25, scalar2=None, op0=ALU.is_gt)
         nc.vector.scalar_tensor_tensor(
             out=part[:, COS], in0=part[:, SIN], scalar=0.25, in1=beyond[:], op0=ALU.add, op1=ALU.subtract
         )
-        trig = keep.tile([P, 2, SETS, PAIRS], F32)
+        trig = keep.tile([P, 3, SETS, PAIRS], F32)
 
         def take_sines():
             nc.scalar.activation(out=trig[:], in_=part[:], func=ACT.Sin, scale=2.0 * math.pi)
@@ -251,16 +252,15 @@ def tile_deepseekv4attention_pa_kernel(
             top[a] = work.tile([P, P], BF16, name="top")
             nc.vector.tensor_max(out=top[a][:], in0=two[a][:, 0, :], in1=two[a][:, 1, :])
 
-        def subtract_top(a, step=SLOTS):
+        def subtract_top(a):
             for half in (LO, HI):
                 width = P - skip(a) if half == LO else P
-                for r in range(0, SLOTS, step):
-                    nc.vector.tensor_tensor(
-                        out=shifted[a][:, SLOTS * half + r : SLOTS * half + r + step, target(a, half)],
-                        in0=gate[a, half][:, r : r + step, source(a, half)],
-                        in1=top[a][:, target(a, half)].unsqueeze(1).to_broadcast([P, step, width]),
-                        op=ALU.subtract,
-                    )
+                nc.vector.tensor_tensor(
+                    out=shifted[a][:, slots(half), target(a, half)],
+                    in0=gate[a, half][:, :, source(a, half)],
+                    in1=top[a][:, target(a, half)].unsqueeze(1).to_broadcast([P, SLOTS, width]),
+                    op=ALU.subtract,
+                )
 
         def weigh(a, half):
             if half == LO:
@@ -330,12 +330,13 @@ def tile_deepseekv4attention_pa_kernel(
             by_cos = work.tile([P, PAIRS, 2], F32, name="by_cos")
             by_sin = work.tile([P, PAIRS, 2], F32, name="by_sin")
             tail = pooled_rows[:, a, P - ROPE : P].rearrange("p (j e) -> p j e", e=2)
-            pair = [P, PAIRS, 2]
-            engine.tensor_tensor(out=by_cos[:], in0=tail, in1=trig[:, COS, a, :].unsqueeze(2).to_broadcast(pair), op=ALU.mult)
-            engine.tensor_tensor(out=by_sin[:], in0=tail, in1=trig[:, SIN, a, :].unsqueeze(2).to_broadcast(pair), op=ALU.mult)
-            spun = rotated_rows[:, a, P - ROPE : P].rearrange("p (j e) -> p j e", e=2)
-            engine.tensor_tensor(out=spun[:, :, 0], in0=by_cos[:, :, 0], in1=by_sin[:, :, 1], op=ALU.subtract)
-            engine.tensor_tensor(out=spun[:, :, 1], in0=by_cos[:, :, 1], in1=by_sin[:, :, 0], op=ALU.add)
+            cosines = trig[:, COS, a, :].unsqueeze(2).to_broadcast([P, PAIRS, 2])
+            signed_sines = trig[:, MINUS_SIN : SIN + 1, a, :].rearrange("p e j -> p j e")
+            engine.tensor_tensor(out=by_cos[:], in0=tail, in1=cosines, op=ALU.mult)
+            engine.tensor_tensor(out=by_sin[:], in0=tail[:, :, ::-1], in1=signed_sines, op=ALU.mult)
+            engine.tensor_tensor(
+                out=rotated_rows[:, a, P - ROPE : P].rearrange("p (j e) -> p j e", e=2), in0=by_cos[:], in1=by_sin[:], op=ALU.add
+            )
 
         def store_rotated(a):
             nc.sync.dma_start(out=out_rotated[:, a, :], in_=rotated_rows[:, a, :])
@@ -351,7 +352,7 @@ def tile_deepseekv4attention_pa_kernel(
         turn_ape()
         quantise(0)
         turn_tokens(1, 0, S)
-        turn_tokens(1, 1, S)
+        turn_tokens(1, 1, V)
         turn_tokens(1, 2, S)
         turn_tokens(1, 3, V)
         quantise(1)
@@ -395,7 +396,7 @@ def tile_deepseekv4attention_pa_kernel(
         max_one(2)
         for s in range(1, SETS):
             a, before = units[s], units[s - 1]
-            subtract_top(a, SLOTS if s + 1 < SETS else 4)
+            subtract_top(a)
             if s + 2 < SETS:
                 project_gates(units[s + 2], LO)
                 project_gates(units[s + 2], HI)
@@ -403,13 +404,14 @@ def tile_deepseekv4attention_pa_kernel(
                 project_kv(LAST)
             weigh(a, LO)
             weigh(a, HI)
-            if before == units[0]:
+            if s + 1 < SETS:
                 invert_joined(before)
             else:
                 invert(before)
             add_and_turn(a, WEIGHTS)
             if s + 2 < SETS:
                 add_offsets(units[s + 2], LO)
+                fetch_weights(a)
                 add_offsets(units[s + 2], HI)
             if s + 1 < SETS:
                 max_four(units[s + 1])

import math
from contextlib import ExitStack

import concourse.mybir as mybir
from concourse.masks import make_identity

F32 = mybir.dt.float32
BF16 = mybir.dt.bfloat16
I32 = mybir.dt.int32
U32 = mybir.dt.uint32
U8 = mybir.dt.uint8
FP8X4 = mybir.dt.float8_e4m3fn_x4
FP4X4 = mybir.dt.float4_e2m1fn_x4
ALU = mybir.AluOpType
ACT = mybir.ActivationFunctionType

P = 128
TOKENS = 2048
HIDDEN = 1024
K_PASS = 512
PASSES = HIDDEN // K_PASS
SLOTS = 4
SETS = 4
ROPE = 64
PAIRS = ROPE // 2
THETA = 10000.0
KV, GATE = 0, 1
LO, HI = 0, 1
WEIGHTS, PRODUCTS = 0, 1
MINUS_SIN, SIN, COS = 0, 1, 2
MASKED = -1.0e30
ROUND_TO_WHOLE = 1.5 * 2.0**23
BLOCK = 8

LAST = 0

FLOPS = 2 * TOKENS * HIDDEN * 4 * P


def tile_deepseekv4attention_pa_kernel(
    tc, hidden, wkv_words, wkv_scales, wgate_words, wgate_scales, ape, out_0, out_1
):
    nc = tc.nc
    with ExitStack() as stack:
        keep = stack.enter_context(tc.tile_pool(name="keep", bufs=1))
        work = stack.enter_context(tc.tile_pool(name="work", bufs=3))
        psum_turn = stack.enter_context(tc.psum_pool(name="psum_turn", bufs=2))
        psum_gate = stack.enter_context(tc.psum_pool(name="psum_gate", bufs=2))
        psum_kv = stack.enter_context(tc.psum_pool(name="psum_kv", bufs=2))
        stack.enter_context(tc.manual_schedule())

        warm = keep.tile([P, 2], F32)
        nc.vector.memset(warm[:], 0.0)
        nc.scalar.activation(out=warm[:, 0:1], in_=warm[:, 1:2], func=ACT.Sin)
        window = keep.tile([P, SETS], F32)
        nc.gpsimd.iota(
            window[:], pattern=[[1, SETS]], base=0, channel_multiplier=SETS, allow_small_or_imprecise_dtypes=True
        )
        ident = keep.tile([P, P], F32)
        make_identity(nc, ident[:])

        freq = keep.tile([P, PAIRS], F32)
        nc.vector.memset(freq[:, 0:1], 1.0)
        have = 1
        while have < PAIRS:
            nc.vector.tensor_scalar_mul(
                out=freq[:, have : 2 * have], in0=freq[:, 0:have], scalar1=THETA ** (-have / PAIRS)
            )
            have *= 2
        table = [P, SETS, PAIRS]
        turns = keep.tile(table, F32)
        nc.vector.scalar_tensor_tensor(
            out=turns[:],
            in0=freq[:].unsqueeze(1).to_broadcast(table),
            scalar=SLOTS / (2.0 * math.pi),
            in1=window[:].unsqueeze(2).to_broadcast(table),
            op0=ALU.mult,
            op1=ALU.mult,
        )
        whole = keep.tile(table, F32)
        nc.vector.tensor_scalar(
            out=whole[:], in0=turns[:], scalar1=ROUND_TO_WHOLE, scalar2=ROUND_TO_WHOLE, op0=ALU.add, op1=ALU.subtract
        )
        part = keep.tile([P, 3, SETS, PAIRS], F32)
        nc.vector.tensor_tensor(out=part[:, SIN], in0=turns[:], in1=whole[:], op=ALU.subtract)
        nc.vector.tensor_tensor(out=part[:, MINUS_SIN], in0=whole[:], in1=turns[:], op=ALU.subtract)
        beyond = keep.tile(table, F32)
        nc.vector.tensor_scalar(out=beyond[:], in0=part[:, SIN], scalar1=0.25, scalar2=None, op0=ALU.is_gt)
        nc.vector.scalar_tensor_tensor(
            out=part[:, COS], in0=part[:, SIN], scalar=0.25, in1=beyond[:], op0=ALU.add, op1=ALU.subtract
        )
        trig = keep.tile([P, 3, SETS, PAIRS], F32)

        def take_sines():
            nc.scalar.activation(out=trig[:], in_=part[:], func=ACT.Sin, scale=2.0 * math.pi)

        def load_exp_table():
            nc.scalar.activation(out=warm[:, 0:1], in_=warm[:, 1:2], func=ACT.Exp)

        rough_skip = keep.tile([P, 2 * SLOTS, P], BF16)
        shifted_skip = keep.tile([P, 2 * SLOTS, P], F32)
        both_skip = keep.tile([P, 2, 2 * SLOTS, P], F32)
        nc.gpsimd.memset(both_skip[:, PRODUCTS, 0:SLOTS, 0:BLOCK], 0.0)
        nc.gpsimd.memset(rough_skip[:, 0:SLOTS, 0 : 2 * BLOCK], MASKED)
        nc.gpsimd.memset(shifted_skip[:, 0:SLOTS, 0:BLOCK], MASKED)

        ape_rows = keep.tile([SLOTS, 2 * P], BF16)
        x = keep.tile([P, SETS * SLOTS, HIDDEN], BF16)
        hidden_rows = hidden.rearrange("b (p i) k -> p (b i) k", i=SETS * SLOTS)

        def load_tokens(i):
            nc.sync.dma_start(out=x[:, i, :], in_=hidden_rows[:, i, :])

        w_words = [keep.tile([P, PASSES, 4 * P], U8, align_bytes=64, name="words_%d" % which) for which in (KV, GATE)]
        w_scales = [keep.tile([P, PASSES, 2 * P], U8, align_bytes=64, name="scales_%d" % which) for which in (KV, GATE)]
        for which in (GATE, KV):
            nc.gpsimd.memset(w_scales[which][:].bitcast(I32), 0)

        def load_weight(which, words, scales):
            nc.sync.dma_start(
                out=w_words[which][:].bitcast(I32), in_=words.bitcast(I32).rearrange("g p b -> p g b")
            )
            rows = scales.bitcast(I32).rearrange("g q n -> q g n")
            for quadrant in range(4):
                nc.sync.dma_start(
                    out=w_scales[which][32 * quadrant : 32 * quadrant + 4, :, :].bitcast(I32),
                    in_=rows[4 * quadrant : 4 * quadrant + 4, :, :],
                )

        for i in range(2):
            load_tokens(i)
        nc.sync.dma_start(out=ape_rows[:], in_=ape)
        for i in range(2, 2 * SLOTS):
            load_tokens(i)
        load_weight(GATE, wgate_words, wgate_scales)
        for i in range(2 * SLOTS, SETS * SLOTS):
            load_tokens(i)
        load_weight(KV, wkv_words, wkv_scales)

        ape_wide = keep.tile([P, 2 * P], F32)
        nc.vector.memset(ape_wide[:], 0.0)
        nc.vector.tensor_copy(out=ape_wide[0:SLOTS, :], in_=ape_rows[:])
        ape_col = keep.tile([P, 2, SLOTS], F32)

        banks_taken = []

        def bank_for_transposes():
            banks_taken.append(1)
            if len(banks_taken) % 2:
                return psum_turn.tile([P, PASSES, 2, P], F32, tag="turn", name="turned")
            return psum_kv.tile([P, PASSES, 2, P], F32, tag="kv", name="turned")

        def turn_ape():
            bank = bank_for_transposes()
            for half in (LO, HI):
                nc.tensor.transpose(bank[:, 0, half, :], ape_wide[:, P * half : P * half + P], ident[:])
            nc.vector.tensor_copy(out=ape_col[:], in_=bank[:, 0, :, 0:SLOTS])

        x_words = x[:].bitcast(F32)
        grouped = keep.tile([P, SETS, PASSES, SLOTS * P, 4], BF16, align_bytes=64)
        grouped_words = grouped[:].bitcast(F32)
        codes = keep.tile([P, SETS, PASSES, SLOTS * P], U32, align_bytes=64)
        planes = keep.tile([P, SETS, PASSES, SLOTS * P], U8, align_bytes=64)

        def turn_tokens(a, r, copy):
            bank = bank_for_transposes()
            for g in range(PASSES):
                for u in range(2):
                    nc.tensor.transpose(
                        bank[:, g, u, :], x_words[:, SLOTS * a + r, 2 * P * g + u : 2 * P * (g + 1) : 2], ident[:]
                    )
            copy(out=grouped_words[:, a, :, P * r : P * (r + 1), :], in_=bank[:].rearrange("q g u p -> q g p u"))

        def quantise(a, first=0, count=SLOTS):
            columns = slice(P * first, P * (first + count))
            for g in range(PASSES):
                nc.vector.quantize_mx(
                    out=codes[:, a, g, columns].bitcast(FP8X4),
                    scales=planes[:, a, g, columns],
                    in_=grouped[:, a, g, columns, :].rearrange("q c t -> q (c t)"),
                )

        def project(pool, which, half, a, tag):
            bank = pool.tile([P, SLOTS, P], F32, tag=tag, name="projected")
            for g in range(PASSES):
                nc.tensor.matmul_mx(
                    out=bank[:].rearrange("f r p -> f (r p)"),
                    lhsT=w_words[which][:, g, 2 * P * half : 2 * P * (half + 1)].bitcast(FP4X4),
                    lhsT_scale=w_scales[which][:, g, P * half : P * (half + 1)],
                    rhs=codes[:, a, g, :].bitcast(FP8X4),
                    rhs_scale=planes[:, a, g, :],
                    start=(g == 0),
                    stop=(g == PASSES - 1),
                )
            return bank

        gate, kv, rough, shifted, four, two, top, both, sums, inverse = {}, {}, {}, {}, {}, {}, {}, {}, {}, {}
        weights, joined = {}, {}
        pooled_rows = keep.tile([P, SETS, P], F32)
        rotated_rows = keep.tile([P, SETS, P], F32)
        out_rotated = out_0.rearrange("b (p a) f -> p (b a) f", a=SETS)
        out_pooled = out_1.rearrange("b (p a) f -> p (b a) f", a=SETS)

        def skip(a):
            return 1 if a == 0 else 0

        def source(a, half):
            return slice(0, P - skip(a)) if half == LO else slice(0, P)

        def target(a, half):
            return slice(skip(a), P) if half == LO else slice(0, P)

        def slots(half):
            return slice(SLOTS * half, SLOTS * (half + 1))

        def project_gates(a, half):
            if half == LO:
                gate[a, LO] = project(psum_gate, GATE, LO, (a - 1) % SETS, "gate_lo")
            else:
                gate[a, HI] = project(psum_gate, GATE, HI, a, "gate_hi")

        def project_kv(a):
            for half in (LO, HI):
                pool, tag = (psum_gate, ("gate_lo", "gate_hi")[half]) if a == LAST else (psum_kv, "kv")
                kv[a, half] = project(pool, KV, half, (a - 1) % SETS if half == LO else a, tag)

        def add_offsets(a, half):
            if half == LO:
                if skip(a):
                    rough[a], shifted[a] = rough_skip, shifted_skip
                else:
                    rough[a] = work.tile([P, 2 * SLOTS, P], BF16, name="rough")
                    shifted[a] = work.tile([P, 2 * SLOTS, P], F32, name="shifted")
            for r in range(SLOTS):
                nc.scalar.activation(
                    out=rough[a][:, SLOTS * half + r, target(a, half)],
                    in_=gate[a, half][:, r, source(a, half)],
                    func=ACT.Identity,
                    bias=ape_col[:, half, r : r + 1],
                    scale=1.0,
                )

        def max_four(a):
            four[a] = work.tile([P, 4, P], BF16, name="four")
            nc.vector.tensor_max(out=four[a][:], in0=rough[a][:, 0:4, :], in1=rough[a][:, 4:8, :])

        def max_two(a):
            two[a] = work.tile([P, 2, P], BF16, name="two")
            nc.vector.tensor_max(out=two[a][:], in0=four[a][:, 0:2, :], in1=four[a][:, 2:4, :])

        def max_one(a):
            top[a] = work.tile([P, P], BF16, name="top")
            nc.vector.tensor_max(out=top[a][:], in0=two[a][:, 0, :], in1=two[a][:, 1, :])

        def subtract_top(a):
            for half in (LO, HI):
                width = P - skip(a) if half == LO else P
                nc.vector.tensor_tensor(
                    out=shifted[a][:, slots(half), target(a, half)],
                    in0=gate[a, half][:, :, source(a, half)],
                    in1=top[a][:, target(a, half)].unsqueeze(1).to_broadcast([P, SLOTS, width]),
                    op=ALU.subtract,
                )

        def weigh(a, half):
            if half == LO:
                both[a] = both_skip if skip(a) else work.tile([P, 2, 2 * SLOTS, P], F32, name="both")
            for r in range(SLOTS):
                nc.scalar.activation(
                    out=both[a][:, WEIGHTS, SLOTS * half + r, :],
                    in_=shifted[a][:, SLOTS * half + r, :],
                    func=ACT.Exp,
                    bias=ape_col[:, half, r : r + 1],
                    scale=1.0,
                )

        def multiply(a, half, step=SLOTS):
            for r in range(0, SLOTS, step):
                some = slice(SLOTS * half + r, SLOTS * half + r + step)
                nc.vector.tensor_tensor(
                    out=both[a][:, PRODUCTS, some, target(a, half)],
                    in0=kv[a, half][:, r : r + step, source(a, half)],
                    in1=both[a][:, WEIGHTS, some, target(a, half)],
                    op=ALU.mult,
                )

        def add_and_turn(a, which):
            if a == LAST:
                bank = psum_kv.tile([P, SLOTS, P], F32, tag="kv", name="sums")
            else:
                bank = psum_turn.tile([P, SLOTS, P], F32, tag="turn", name="sums")
            sums[a, which] = bank[:, 0, :]
            for s in range(2 * SLOTS):
                nc.tensor.matmul(
                    out=sums[a, which],
                    lhsT=both[a][:, which, s, :],
                    rhs=ident[:],
                    start=(s == 0),
                    stop=(s == 2 * SLOTS - 1),
                    is_transpose=True,
                )

        def fetch_weights(a):
            weights[a] = work.tile([P, 2, P // 2], F32, name="weights")
            nc.scalar.copy(out=weights[a][:].rearrange("p h f -> p (h f)"), in_=sums[a, WEIGHTS])
            joined[a] = work.tile([P, P // 2], F32, name="joined")
            nc.gpsimd.tensor_tensor(out=joined[a][:], in0=weights[a][:, 0], in1=weights[a][:, 1], op=ALU.mult)

        def invert_joined(a):
            shared = work.tile([P, P // 2], F32, name="shared")
            nc.vector.reciprocal(out=shared[:], in_=joined[a][:])
            inverse[a] = work.tile([P, 2, P // 2], F32, name="inverse")
            nc.gpsimd.tensor_tensor(
                out=inverse[a][:],
                in0=weights[a][:, ::-1, :],
                in1=shared[:].unsqueeze(1).to_broadcast([P, 2, P // 2]),
                op=ALU.mult,
            )

        def invert(a):
            inverse[a] = work.tile([P, 2, P // 2], F32, name="inverse")
            nc.vector.reciprocal(out=inverse[a][:].rearrange("p h f -> p (h f)"), in_=sums[a, WEIGHTS])

        def divide(a):
            nc.vector.tensor_tensor(out=pooled_rows[:, a, :], in0=sums[a, PRODUCTS], in1=inverse[a][:].rearrange("p h f -> p (h f)"), op=ALU.mult)
            nc.sync.dma_start(out=out_pooled[:, a, :], in_=pooled_rows[:, a, :])

        def rotate(a, engine):
            nc.scalar.copy(out=rotated_rows[:, a, 0 : P - ROPE], in_=pooled_rows[:, a, 0 : P - ROPE])
            by_cos = work.tile([P, PAIRS, 2], F32, name="by_cos")
            by_sin = work.tile([P, PAIRS, 2], F32, name="by_sin")
            tail = pooled_rows[:, a, P - ROPE : P].rearrange("p (j e) -> p j e", e=2)
            cosines = trig[:, COS, a, :].unsqueeze(2).to_broadcast([P, PAIRS, 2])
            signed_sines = trig[:, MINUS_SIN : SIN + 1, a, :].rearrange("p e j -> p j e")
            engine.tensor_tensor(out=by_cos[:], in0=tail, in1=cosines, op=ALU.mult)
            engine.tensor_tensor(out=by_sin[:], in0=tail[:, :, ::-1], in1=signed_sines, op=ALU.mult)
            engine.tensor_tensor(
                out=rotated_rows[:, a, P - ROPE : P].rearrange("p (j e) -> p j e", e=2), in0=by_cos[:], in1=by_sin[:], op=ALU.add
            )

        def store_rotated(a):
            nc.sync.dma_start(out=out_rotated[:, a, :], in_=rotated_rows[:, a, :])

        units = [1, 2, 3, 0]
        V, S = nc.vector.tensor_copy, nc.scalar.copy
        turn_tokens(0, 0, S)
        turn_tokens(0, 1, V)
        turn_tokens(0, 2, S)
        turn_tokens(0, 3, V)
        take_sines()
        load_exp_table()
        turn_ape()
        quantise(0)
        turn_tokens(1, 0, S)
        turn_tokens(1, 1, V)
        turn_tokens(1, 2, S)
        turn_tokens(1, 3, V)
        quantise(1)
        project_gates(1, LO)
        add_offsets(1, LO)
        turn_tokens(2, 0, S)
        turn_tokens(2, 1, S)
        turn_tokens(2, 2, S)
        turn_tokens(2, 3, V)
        project_gates(1, HI)
        add_offsets(1, HI)
        quantise(2)
        turn_tokens(3, 0, V)
        turn_tokens(3, 1, S)
        turn_tokens(3, 2, S)
        turn_tokens(3, 3, S)
        project_gates(2, LO)
        add_offsets(2, LO)
        project_gates(2, HI)
        project_kv(1)
        max_four(1)
        max_two(1)
        max_one(1)
        subtract_top(1)
        weigh(1, LO)
        add_offsets(2, HI)
        weigh(1, HI)
        quantise(3)
        multiply(1, LO)
        max_four(2)
        max_two(2)
        multiply(1, HI)
        project_gates(3, LO)
        project_gates(3, HI)
        add_and_turn(1, WEIGHTS)
        add_offsets(3, LO)
        fetch_weights(1)
        add_offsets(3, HI)
        project_kv(2)
        add_and_turn(1, PRODUCTS)
        max_one(2)
        for s in range(1, SETS):
            a, before = units[s], units[s - 1]
            subtract_top(a)
            if s + 2 < SETS:
                project_gates(units[s + 2], LO)
                project_gates(units[s + 2], HI)
            elif s + 1 < SETS:
                project_kv(LAST)
            weigh(a, LO)
            weigh(a, HI)
            if s + 1 < SETS:
                invert_joined(before)
            else:
                invert(before)
            add_and_turn(a, WEIGHTS)
            if s + 2 < SETS:
                add_offsets(units[s + 2], LO)
                fetch_weights(a)
                add_offsets(units[s + 2], HI)
            if s + 1 < SETS:
                max_four(units[s + 1])
            multiply(a, LO, SLOTS if s + 1 < SETS else 2)
            if s + 1 < SETS:
                max_two(units[s + 1])
            if s + 1 == SETS:
                divide(before)
                rotate(before, nc.gpsimd)
            multiply(a, HI, SLOTS if s + 1 < SETS else 2)
            if s + 2 < SETS:
                project_kv(units[s + 1])
            add_and_turn(a, PRODUCTS)
            if s + 1 < SETS:
                max_one(units[s + 1])
            if s + 1 < SETS:
                divide(before)
                rotate(before, nc.gpsimd)
                store_rotated(before)
        invert(LAST)
        divide(LAST)
        store_rotated(units[SETS - 2])
        rotate(LAST, nc.vector)
        store_rotated(LAST)
